import numpy as np
import ml_dtypes


def mxq(x, axis, fmt="e4m3"):
    dtype, down = {"e4m3": (ml_dtypes.float8_e4m3fn, 7), "e5m2": (ml_dtypes.float8_e5m2, 14)}[fmt]
    v = np.moveaxis(np.asarray(x, np.float32).astype(ml_dtypes.bfloat16).astype(np.float64), axis, -1)
    blocks = v.reshape(v.shape[:-1] + (-1, 32))
    amax = np.abs(blocks).max(-1, keepdims=True)
    byte = np.maximum(np.where(amax > 0, np.frexp(amax)[1] - 1 + 127, 0) - down, 1)
    scale = np.exp2(byte - 127.0)
    codes = (blocks / scale).astype(np.float32).astype(dtype).astype(np.float64)
    return np.moveaxis((codes * scale).reshape(v.shape), -1, axis)


WIDE = False


def mx_kscale(k):
    if not WIDE:
        return np.ones(k)
    levels = np.array([10, -10, 5, -5, 0])
    if k % 512:
        return np.exp2(np.random.permutation(np.resize(levels, k // 32))).repeat(32)
    a = np.empty((k // 512, 16))
    for p in range(k // 512):
        a[p, :8] = np.random.permutation(np.resize(levels, 8))
        for g in range(8):
            far = levels[np.abs(levels - a[p, g]) >= 10]
            a[p, g + 8] = far[np.random.randint(len(far))]
    return np.exp2(a.ravel()).repeat(32)


BF16 = ml_dtypes.bfloat16


def bf(x):
    return np.asarray(x, np.float32).astype(BF16)


def f64(x):
    return np.asarray(x).astype(np.float64)


N, H, W, K = 512, 2048, 8, 512
TAU = 1.0


def silu(v):
    return v / (1.0 + np.exp(-v))


def softmax_last(v):
    e = np.exp(v - v.max(-1, keepdims=True))
    return e / e.sum(-1, keepdims=True)


def draw0():
    s = np.tile(mx_kscale(K), W)
    return {"x": bf(np.random.standard_normal((N, W * K)) * s),
            "template_flat": bf(np.random.standard_normal((H, W * K)) / np.sqrt(K) / s)}


def core(x, template_flat):
    n = x.shape[0]
    h = template_flat.shape[0]
    xw = f64(x).reshape(n, W, K)
    tw = f64(template_flat).reshape(h, W, K)
    xq = mxq(xw, 2, "e4m3")
    tq = mxq(tw, 2, "e4m3")
    s = (xq.transpose(1, 0, 2) @ tq.transpose(1, 2, 0)).transpose(1, 2, 0)
    gate = softmax_last(s / TAU)
    return np.sum(gate * silu(s), axis=-1)


def e4m3fn_bytes(y):
    return np.clip(np.asarray(y, np.float64), -448.0, 448.0).astype(np.float32).astype(ml_dtypes.float8_e4m3fn).view(np.uint8)


def e4m3fn_values(b):
    return np.asarray(b, np.uint8).view(ml_dtypes.float8_e4m3fn).astype(np.float64)


def setup_inputs():
    d = draw0()
    x0 = np.asarray(d['template_flat']).astype(np.float64)
    s = (np.max(np.abs(x0), axis=(0,), keepdims=True) / 448.0).astype(np.float32)
    out = {}
    for k, v in d.items():
        if k == 'template_flat':
            out['template_flat_bytes'] = e4m3fn_bytes(x0 / s.astype(np.float64))
            out['template_flat_scale'] = s
        else:
            out[k] = v
    return out


def reference(x, template_flat_bytes, template_flat_scale):
    return core(x, e4m3fn_values(template_flat_bytes) * template_flat_scale.astype(np.float64))

@@ -1,0 +1,303 @@
+from contextlib import ExitStack
+
+import concourse.mybir as mybir
+from concourse.masks import make_identity
+
+N = 512
+H = 2048
+W = 8
+K = 512
+P = 128
+FLOPS = 2 * N * H * W * K
+
+F32 = mybir.dt.float32
+BF16 = mybir.dt.bfloat16
+U32 = mybir.dt.uint32
+U8 = mybir.dt.uint8
+FP8 = mybir.dt.float8_e4m3fn
+FP8X4 = mybir.dt.float8_e4m3fn_x4
+ACT = mybir.ActivationFunctionType
+ALU = mybir.AluOpType
+
+HT = H // P
+NT = N // P
+BATCH = 2
+BURST = 4
+NB = HT // BATCH
+
+
+def tile_dendriticlayersilu_ffn_kernel(tc, x, template_flat_bytes, template_flat_scale, out):
+    nc = tc.nc
+    with ExitStack() as ctx:
+        keep = ctx.enter_context(tc.tile_pool(name="keep", bufs=1))
+        stage = ctx.enter_context(tc.tile_pool(name="stage", bufs=2))
+        work = ctx.enter_context(tc.tile_pool(name="work", bufs=3))
+        small = ctx.enter_context(tc.tile_pool(name="small", bufs=2))
+        psum = ctx.enter_context(tc.psum_pool(name="psum", bufs=5))
+        ctx.enter_context(tc.manual_schedule(engines={mybir.EngineType.Activation, mybir.EngineType.DVE, mybir.EngineType.Pool, mybir.EngineType.PE}))
+
+        ident = keep.tile([P, P], F32, name="ident")
+        make_identity(nc, ident[:])
+        x_codes = keep.tile([P, W * N], U32, name="x_codes", align_bytes=64)
+        x_scales = keep.tile([P, W * N], U8, name="x_scales", align_bytes=64)
+        scale_bc = keep.tile([P, W * K], F32, name="scale_bc")
+        seen_by_vector = keep.tile([P, 1], F32, name="seen_by_vector")
+        seen_by_gpsimd = keep.tile([P, 1], U32, name="seen_by_gpsimd")
+
+        out_view = out.rearrange("(nb p) h -> p nb h", p=P)
+        x_view = x.rearrange("(i p) k -> p i k", p=P)
+        batches = [list(range(b * BATCH, (b + 1) * BATCH)) for b in range(NB)]
+        tb = {}
+        wb = {}
+        grouped = {}
+        t_codes = {}
+        t_scales = {}
+        run = {}
+        f = {}
+        d = {}
+        acc_d = {}
+        acc_n = {}
+        ln_d = {}
+        r_d = {}
+
+        def load_bytes(t):
+            tb[t] = stage.tile([P, W * K], U8, name="tb", bufs=4)
+            nc.sync.dma_start(out=tb[t][:], in_=template_flat_bytes[t * P : (t + 1) * P, :])
+
+        def widen(t):
+            wb[t] = stage.tile([P, W * K], BF16, name="wb", bufs=3)
+            for c in range(2):
+                cs = slice(c * 2048, (c + 1) * 2048)
+                nc.vector.tensor_tensor(
+                    out=wb[t][:, cs], in0=tb[t][:, cs].bitcast(FP8), in1=scale_bc[:, cs], op=ALU.mult
+                )
+
+        def turn(words, dst, on_vector=False):
+            for q in range(W // 2):
+                bank = psum.tile([P, 2, 2, P], F32, name="rot")
+                for gg in range(2):
+                    g = 2 * q + gg
+                    for u in range(2):
+                        nc.tensor.transpose(bank[:, gg, u, :], words[:, 256 * g + u : 256 * (g + 1) : 2], ident[:])
+                if on_vector:
+                    nc.vector.tensor_copy(out=dst(q), in_=bank[:].rearrange("p g u r -> p g r u"))
+                else:
+                    nc.scalar.copy(out=dst(q), in_=bank[:].rearrange("p g u r -> p g r u"))
+
+        def evac(t, on_vector=False):
+            grouped[t] = stage.tile([P, W * K], BF16, name="grouped", bufs=2, align_bytes=64)
+            g_words = grouped[t][:].bitcast(F32).rearrange("p (g r u) -> p g r u", g=W, u=2)
+            turn(wb[t][:].bitcast(F32), lambda q: g_words[:, 2 * q : 2 * q + 2, :, :], on_vector)
+
+        def quant(t):
+            t_codes[t] = stage.tile([P, W * P], U32, name="t_codes", bufs=4, align_bytes=64)
+            t_scales[t] = stage.tile([P, W * P], U8, name="t_scales", bufs=4, align_bytes=64)
+            nc.vector.quantize_mx(out=t_codes[t][:].bitcast(FP8X4), scales=t_scales[t][:], in_=grouped[t][:])
+
+        def scores(bank, t, w):
+            nc.tensor.matmul_mx(
+                out=bank[:],
+                lhsT=t_codes[t][:, w * P : (w + 1) * P].bitcast(FP8X4),
+                lhsT_scale=t_scales[t][:, w * P : (w + 1) * P],
+                rhs=x_codes[:, w * N : (w + 1) * N].bitcast(FP8X4),
+                rhs_scale=x_scales[:, w * N : (w + 1) * N],
+                start=True,
+                stop=True,
+            )
+
+        def units(todo):
+            for kind, t, nb in todo:
+                if t < 0 or t >= HT:
+                    continue
+                if kind == "d":
+                    if nb == 0:
+                        acc_d[t] = psum.tile([P, N], F32, name="acc", bufs=3)
+                    window_sum(acc_d[t], d[t], nb)
+                else:
+                    if nb == 0:
+                        acc_n[t] = psum.tile([P, N], F32, name="acc", bufs=3)
+                    window_sum(acc_n[t], f[t], nb)
+
+        def max_pass(tiles, between):
+            for t in tiles:
+                run[t] = small.tile([P, N], F32, name="run", bufs=4)
+            order = [(t, w) for w in range(W) for t in tiles]
+            for i in range(len(order) // BURST):
+                part = order[i * BURST : (i + 1) * BURST]
+                banks = []
+                for t, w in part:
+                    bank = psum.tile([P, N], F32, name="rot")
+                    scores(bank, t, w)
+                    banks.append(bank)
+                for (t, w), bank in zip(part, banks):
+                    if w == 0:
+                        nc.vector.tensor_copy(out=run[t][:], in_=bank[:])
+                    else:
+                        nc.vector.tensor_tensor(out=run[t][:], in0=bank[:], in1=run[t][:], op=ALU.max)
+                units(between[i])
+
+        def sub_silu(tiles, between):
+            order = [(t, w) for t in tiles for w in range(W)]
+            for i in range(len(order) // BURST):
+                part = order[i * BURST : (i + 1) * BURST]
+                banks = []
+                for t, w in part:
+                    if w == 0:
+                        f[t] = work.tile([P, W, N], F32, name="f", align_bytes=64)
+                        d[t] = work.tile([P, W, N], F32, name="d", align_bytes=64)
+                    bank = psum.tile([P, N], F32, name="rot")
+                    scores(bank, t, w)
+                    banks.append(bank)
+                for (t, w), bank in zip(part, banks):
+                    nc.scalar.activation(out=f[t][:, w, :], in_=bank[:], func=ACT.Silu)
+                    nc.vector.tensor_tensor(out=d[t][:, w, :], in0=bank[:], in1=run[t][:], op=ALU.subtract)
+                units(between[i])
+
+        def exp_pass(t):
+            for c in range(2):
+                cs = slice(c * 256, (c + 1) * 256)
+                nc.scalar.activation(out=d[t][:, :, cs], in_=d[t][:, :, cs], func=ACT.Exp)
+
+        def window_sum(acc, src, nb):
+            bs = slice(nb * P, (nb + 1) * P)
+            for w in range(W):
+                nc.tensor.matmul(
+                    out=acc[:, bs],
+                    lhsT=src[:, w, bs],
+                    rhs=ident[:],
+                    is_transpose=True,
+                    start=(w == 0),
+                    stop=(w == W - 1),
+                )
+
+        def log_pass(tiles):
+            for t in tiles:
+                ln_d[t] = small.tile([P, N], F32, name="ln_d")
+                nc.scalar.activation(out=ln_d[t][:], in_=acc_d[t][:], func=ACT.Ln)
+
+        def recip_pass(tiles):
+            for t in tiles:
+                r_d[t] = small.tile([P, N], F32, name="r_d")
+                nc.scalar.activation(out=r_d[t][:], in_=ln_d[t][:], func=ACT.Exp, scale=-1.0)
+
+        def finish(t):
+            o = small.tile([P, N], F32, name="o")
+            nc.vector.tensor_tensor(out=o[:], in0=acc_n[t][:], in1=r_d[t][:], op=ALU.mult)
+            nc.sync.dma_start(out=out_view[:, :, t * P : (t + 1) * P], in_=o[:].rearrange("p (nb h) -> p nb h", nb=NT))
+
+        x_rows = []
+
+        def load_x(a):
+            xr = work.tile([P, 2, W * K], BF16, name="d", align_bytes=64)
+            nc.sync.dma_start(out=xr[:], in_=x_view[:, 2 * a : 2 * a + 2, :])
+            x_rows.append(xr)
+
+        load_bytes(0)
+        for c in range(2):
+            cs = slice(c * 2048, (c + 1) * 2048)
+            nc.sync.dma_start(
+                out=scale_bc[:, cs], in_=template_flat_scale[:, cs].rearrange("o k -> (o k)").partition_broadcast(P)
+            )
+        load_bytes(1)
+        load_bytes(2)
+        load_x(0)
+        load_bytes(3)
+        load_x(1)
+        widen(0)
+        widen(1)
+        load_bytes(4)
+        load_bytes(5)
+        x_grouped = []
+        xg_words = []
+        for a in range(2):
+            xg = work.tile([P, 4 * N * 4], BF16, name="f", align_bytes=64)
+            x_grouped.append(xg)
+            xg_words.append(xg[:].bitcast(F32).rearrange("p (g n u) -> p g n u", g=4, u=2))
+
+        def turn_x(i):
+            turn(
+                x_rows[i // 2][:, i % 2, :].bitcast(F32),
+                lambda q: xg_words[q // 2][:, 2 * (q % 2) : 2 * (q % 2) + 2, i * P : (i + 1) * P, :],
+            )
+
+        evac(0)
+        turn_x(0)
+        evac(1)
+        turn_x(1)
+        turn_x(2)
+        turn_x(3)
+        widen(2)
+        widen(3)
+        quant(0)
+        quant(1)
+        for a in range(2):
+            for c in range(2):
+                g = 4 * a + 2 * c
+                nc.vector.quantize_mx(
+                    out=x_codes[:, g * N : (g + 2) * N].bitcast(FP8X4),
+                    scales=x_scales[:, g * N : (g + 2) * N],
+                    in_=x_grouped[a][:, c * 4096 : (c + 1) * 4096],
+                )
+        max_pass(batches[0], [[], [], [], []])
+
+        for b in range(NB):
+            cur = batches[b]
+            t0 = cur[0]
+            if b + 3 < NB:
+                for t in batches[b + 3]:
+                    load_bytes(t)
+            sub_silu(
+                cur,
+                [
+                    [("n", t0 - 2, 2)],
+                    [("n", t0 - 2, 3), ("d", t0 - 1, 0)],
+                    [("d", t0 - 1, 1), ("d", t0 - 1, 2)],
+                    [("d", t0 - 1, 3)],
+                ],
+            )
+            if b >= 1:
+                log_pass(batches[b - 1])
+            if b + 2 < NB:
+                if b >= 1:
+                    nc.vector.tensor_copy(out=seen_by_vector[:], in_=f[t0 - 1][:, W - 1, N - 1 : N])
+                for t in batches[b + 2]:
+                    widen(t)
+            for i in range(BATCH):
+                if b + 1 < NB:
+                    evac(batches[b + 1][i], on_vector=(b + 2 >= NB))
+                units([("n", t0 - 1, 2 * i), ("n", t0 - 1, 2 * i + 1)])
+            if b + 1 < NB:
+                for t in batches[b + 1]:
+                    quant(t)
+            if b >= 1:
+                recip_pass(batches[b - 1])
+                for t in batches[b - 1]:
+                    finish(t)
+            for t in cur:
+                exp_pass(t)
+            if b + 1 < NB:
+                nc.gpsimd.tensor_copy(out=seen_by_gpsimd[:], in_=t_codes[t0 + 3][:, W * P - 1 : W * P])
+                for t in cur:
+                    for nb in range(NT):
+                        bs = slice(nb * P, (nb + 1) * P)
+                        nc.gpsimd.tensor_tensor(out=f[t][:, :, bs], in0=f[t][:, :, bs], in1=d[t][:, :, bs], op=ALU.mult)
+                max_pass(
+                    batches[b + 1],
+                    [
+                        [],
+                        [("d", t0, 0), ("d", t0, 1)],
+                        [("d", t0, 2), ("d", t0, 3)],
+                        [("n", t0, 0), ("n", t0, 1)],
+                    ],
+                )
+            else:
+                for t in cur:
+                    units([("d", t, nb) for nb in range(NT)])
+                    for nb in range(NT):
+                        bs = slice(nb * P, (nb + 1) * P)
+                        nc.vector.tensor_tensor(out=f[t][:, :, bs], in0=f[t][:, :, bs], in1=d[t][:, :, bs], op=ALU.mult)
+                        units([("n", t, nb)])
+        log_pass(batches[NB - 1])
+        recip_pass(batches[NB - 1])
+        for t in batches[NB - 1]:
+            finish(t)

@@ -250,13 +250,13 @@ def tile_dendriticlayersilu_ffn_kernel(tc, x, template_flat_bytes, template_flat
                 cur,
                 [
                     [("n", t0 - 2, 2)],
-                    [("n", t0 - 2, 3), ("d", t0 - 1, 0)],
-                    [("d", t0 - 1, 1), ("d", t0 - 1, 2)],
-                    [("d", t0 - 1, 3)],
+                    [("n", t0 - 2, 3)],
+                    [],
+                    [],
                 ],
             )
             if b >= 1:
-                log_pass(batches[b - 1])
+                log_pass([t0 - 2])
             if b + 2 < NB:
                 if b >= 1:
                     nc.vector.tensor_copy(out=seen_by_vector[:], in_=f[t0 - 1][:, W - 1, N - 1 : N])
@@ -265,11 +265,12 @@ def tile_dendriticlayersilu_ffn_kernel(tc, x, template_flat_bytes, template_flat
             for i in range(BATCH):
                 if b + 1 < NB:
                     evac(batches[b + 1][i], on_vector=(b + 2 >= NB))
-                units([("n", t0 - 1, 2 * i), ("n", t0 - 1, 2 * i + 1)])
+                units([(("d", "n")[i], t0 - 1, nb) for nb in range(NT)])
             if b + 1 < NB:
                 for t in batches[b + 1]:
                     quant(t)
             if b >= 1:
+                log_pass([t0 - 1])
                 recip_pass(batches[b - 1])
                 for t in batches[b - 1]:
                     finish(t)

@@ -180,6 +180,10 @@ def tile_dendriticlayersilu_ffn_kernel(tc, x, template_flat_bytes, template_flat
                 r_d[t] = small.tile([P, N], F32, name="r_d")
                 nc.scalar.activation(out=r_d[t][:], in_=ln_d[t][:], func=ACT.Exp, scale=-1.0)
 
+        def divide(t):
+            r_d[t] = small.tile([P, N], F32, name="r_d")
+            nc.vector.reciprocal(out=r_d[t][:], in_=acc_d[t][:])
+
         def finish(t):
             o = small.tile([P, N], F32, name="o")
             nc.vector.tensor_tensor(out=o[:], in0=acc_n[t][:], in1=r_d[t][:], op=ALU.mult)
@@ -255,7 +259,10 @@ def tile_dendriticlayersilu_ffn_kernel(tc, x, template_flat_bytes, template_flat
                     [],
                 ],
             )
-            if b >= 1:
+            if b + 1 >= NB:
+                divide(t0 - 2)
+                finish(t0 - 2)
+            elif b >= 1:
                 log_pass([t0 - 2])
             if b + 2 < NB:
                 if b >= 1:
@@ -269,7 +276,10 @@ def tile_dendriticlayersilu_ffn_kernel(tc, x, template_flat_bytes, template_flat
             if b + 1 < NB:
                 for t in batches[b + 1]:
                     quant(t)
-            if b >= 1:
+            if b + 1 >= NB:
+                divide(t0 - 1)
+                finish(t0 - 1)
+            elif b >= 1:
                 log_pass([t0 - 1])
                 recip_pass(batches[b - 1])
                 for t in batches[b - 1]:
@@ -292,11 +302,14 @@ def tile_dendriticlayersilu_ffn_kernel(tc, x, template_flat_bytes, template_flat
                     ],
                 )
             else:
+                units([("d", cur[0], nb) for nb in range(NT)])
                 for t in cur:
-                    units([("d", t, nb) for nb in range(NT)])
                     for nb in range(NT):
+                        if t == cur[0] and nb == NT - 1:
+                            units([("d", cur[1], k) for k in range(NT)])
                         bs = slice(nb * P, (nb + 1) * P)
-                        nc.vector.tensor_tensor(out=f[t][:, :, bs], in0=f[t][:, :, bs], in1=d[t][:, :, bs], op=ALU.mult)
+                        engine = nc.gpsimd if (t == cur[0] and nb < 2) else nc.vector
+                        engine.tensor_tensor(out=f[t][:, :, bs], in0=f[t][:, :, bs], in1=d[t][:, :, bs], op=ALU.mult)
                         units([("n", t, nb)])
         log_pass(batches[NB - 1])
         recip_pass(batches[NB - 1])

@@ -72,22 +72,22 @@ def tile_dendriticlayersilu_ffn_kernel(tc, x, template_flat_bytes, template_flat
                     out=wb[t][:, cs], in0=tb[t][:, cs].bitcast(FP8), in1=scale_bc[:, cs], op=ALU.mult
                 )
 
-        def turn(words, dst, on_vector=False):
+        def turn(words, dst, vector_from=W // 2):
             for q in range(W // 2):
                 bank = psum.tile([P, 2, 2, P], F32, name="rot")
                 for gg in range(2):
                     g = 2 * q + gg
                     for u in range(2):
                         nc.tensor.transpose(bank[:, gg, u, :], words[:, 256 * g + u : 256 * (g + 1) : 2], ident[:])
-                if on_vector:
+                if q >= vector_from:
                     nc.vector.tensor_copy(out=dst(q), in_=bank[:].rearrange("p g u r -> p g r u"))
                 else:
                     nc.scalar.copy(out=dst(q), in_=bank[:].rearrange("p g u r -> p g r u"))
 
-        def evac(t, on_vector=False):
+        def evac(t, vector_from=W // 2):
             grouped[t] = stage.tile([P, W * K], BF16, name="grouped", bufs=2, align_bytes=64)
             g_words = grouped[t][:].bitcast(F32).rearrange("p (g r u) -> p g r u", g=W, u=2)
-            turn(wb[t][:].bitcast(F32), lambda q: g_words[:, 2 * q : 2 * q + 2, :, :], on_vector)
+            turn(wb[t][:].bitcast(F32), lambda q: g_words[:, 2 * q : 2 * q + 2, :, :], vector_from)
 
         def quant(t):
             t_codes[t] = stage.tile([P, W * P], U32, name="t_codes", bufs=4, align_bytes=64)
@@ -271,8 +271,9 @@ def tile_dendriticlayersilu_ffn_kernel(tc, x, template_flat_bytes, template_flat
                     widen(t)
             for i in range(BATCH):
                 if b + 1 < NB:
-                    evac(batches[b + 1][i], on_vector=(b + 2 >= NB))
-                units([(("d", "n")[i], t0 - 1, nb) for nb in range(NT)])
+                    evac(batches[b + 1][i], vector_from=(0 if b + 2 >= NB else W // 2 - i))
+                units([("d", t0 - 1, 2 * i), ("d", t0 - 1, 2 * i + 1)])
+            units([("n", t0 - 1, nb) for nb in range(NT)])
             if b + 1 < NB:
                 for t in batches[b + 1]:
                     quant(t)

@@ -72,8 +72,17 @@ def tile_dendriticlayersilu_ffn_kernel(tc, x, template_flat_bytes, template_flat
                     out=wb[t][:, cs], in0=tb[t][:, cs].bitcast(FP8), in1=scale_bc[:, cs], op=ALU.mult
                 )
 
-        def turn(words, dst, vector_from=W // 2):
-            for q in range(W // 2):
+        def cast(t):
+            wb[t] = stage.tile([P, W * K], BF16, name="wb", bufs=3)
+            nc.vector.tensor_copy(out=wb[t][:], in_=tb[t][:].bitcast(FP8))
+
+        def scale_on_gpsimd(t):
+            for c in range(2):
+                cs = slice(c * 2048, (c + 1) * 2048)
+                nc.gpsimd.tensor_tensor(out=wb[t][:, cs], in0=wb[t][:, cs], in1=scale_bc[:, cs], op=ALU.mult)
+
+        def turn(words, dst, banks=W // 2, vector_from=W // 2):
+            for q in range(banks):
                 bank = psum.tile([P, 2, 2, P], F32, name="rot")
                 for gg in range(2):
                     g = 2 * q + gg
@@ -87,7 +96,7 @@ def tile_dendriticlayersilu_ffn_kernel(tc, x, template_flat_bytes, template_flat
         def evac(t, vector_from=W // 2):
             grouped[t] = stage.tile([P, W * K], BF16, name="grouped", bufs=2, align_bytes=64)
             g_words = grouped[t][:].bitcast(F32).rearrange("p (g r u) -> p g r u", g=W, u=2)
-            turn(wb[t][:].bitcast(F32), lambda q: g_words[:, 2 * q : 2 * q + 2, :, :], vector_from)
+            turn(wb[t][:].bitcast(F32), lambda q: g_words[:, 2 * q : 2 * q + 2, :, :], vector_from=vector_from)
 
         def quant(t):
             t_codes[t] = stage.tile([P, W * P], U32, name="t_codes", bufs=4, align_bytes=64)
@@ -189,12 +198,12 @@ def tile_dendriticlayersilu_ffn_kernel(tc, x, template_flat_bytes, template_flat
             nc.vector.tensor_tensor(out=o[:], in0=acc_n[t][:], in1=r_d[t][:], op=ALU.mult)
             nc.sync.dma_start(out=out_view[:, :, t * P : (t + 1) * P], in_=o[:].rearrange("p (nb h) -> p nb h", nb=NT))
 
-        x_rows = []
+        x_cols = []
 
         def load_x(a):
-            xr = work.tile([P, 2, W * K], BF16, name="d", align_bytes=64)
-            nc.sync.dma_start(out=xr[:], in_=x_view[:, 2 * a : 2 * a + 2, :])
-            x_rows.append(xr)
+            xc = work.tile([P, NT, 4 * K], BF16, name="d", align_bytes=64)
+            nc.sync.dma_start(out=xc[:], in_=x_view[:, :, a * 4 * K : (a + 1) * 4 * K])
+            x_cols.append(xc)
 
         load_bytes(0)
         for c in range(2):
@@ -203,14 +212,16 @@ def tile_dendriticlayersilu_ffn_kernel(tc, x, template_flat_bytes, template_flat
                 out=scale_bc[:, cs], in_=template_flat_scale[:, cs].rearrange("o k -> (o k)").partition_broadcast(P)
             )
         load_bytes(1)
-        load_bytes(2)
         load_x(0)
+        load_bytes(2)
         load_bytes(3)
         load_x(1)
         widen(0)
         widen(1)
         load_bytes(4)
         load_bytes(5)
+        cast(2)
+        cast(3)
         x_grouped = []
         xg_words = []
         for a in range(2):
@@ -218,23 +229,13 @@ def tile_dendriticlayersilu_ffn_kernel(tc, x, template_flat_bytes, template_flat
             x_grouped.append(xg)
             xg_words.append(xg[:].bitcast(F32).rearrange("p (g n u) -> p g n u", g=4, u=2))
 
-        def turn_x(i):
-            turn(
-                x_rows[i // 2][:, i % 2, :].bitcast(F32),
-                lambda q: xg_words[q // 2][:, 2 * (q % 2) : 2 * (q % 2) + 2, i * P : (i + 1) * P, :],
-            )
-
-        evac(0)
-        turn_x(0)
-        evac(1)
-        turn_x(1)
-        turn_x(2)
-        turn_x(3)
-        widen(2)
-        widen(3)
-        quant(0)
-        quant(1)
-        for a in range(2):
+        def prepare_x(a):
+            for i in range(NT):
+                turn(
+                    x_cols[a][:, i, :].bitcast(F32),
+                    lambda q: xg_words[a][:, 2 * q : 2 * q + 2, i * P : (i + 1) * P, :],
+                    banks=2,
+                )
             for c in range(2):
                 g = 4 * a + 2 * c
                 nc.vector.quantize_mx(
@@ -242,6 +243,14 @@ def tile_dendriticlayersilu_ffn_kernel(tc, x, template_flat_bytes, template_flat
                     scales=x_scales[:, g * N : (g + 2) * N],
                     in_=x_grouped[a][:, c * 4096 : (c + 1) * 4096],
                 )
+
+        for a in range(2):
+            evac(a)
+            quant(a)
+            prepare_x(a)
+        nc.gpsimd.tensor_copy(out=seen_by_gpsimd[:], in_=x_codes[:, W * N - 1 : W * N])
+        scale_on_gpsimd(2)
+        scale_on_gpsimd(3)
         max_pass(batches[0], [[], [], [], []])
 
         for b in range(NB):
@@ -267,6 +276,8 @@ def tile_dendriticlayersilu_ffn_kernel(tc, x, template_flat_bytes, template_flat
             if b + 2 < NB:
                 if b >= 1:
                     nc.vector.tensor_copy(out=seen_by_vector[:], in_=f[t0 - 1][:, W - 1, N - 1 : N])
+                else:
+                    nc.vector.tensor_copy(out=seen_by_vector[:], in_=wb[3][:, W * K - 1 : W * K])
                 for t in batches[b + 2]:
                     widen(t)
             for i in range(BATCH):

@@ -83,15 +83,15 @@ def tile_dendriticlayersilu_ffn_kernel(tc, x, template_flat_bytes, template_flat
 
         def turn(words, dst, banks=W // 2, vector_from=W // 2):
             for q in range(banks):
-                bank = psum.tile([P, 2, 2, P], F32, name="rot")
+                bank = psum.tile([P, 2, P, 2], F32, name="rot")
                 for gg in range(2):
                     g = 2 * q + gg
                     for u in range(2):
-                        nc.tensor.transpose(bank[:, gg, u, :], words[:, 256 * g + u : 256 * (g + 1) : 2], ident[:])
+                        nc.tensor.transpose(bank[:, gg, :, u], words[:, 256 * g + u : 256 * (g + 1) : 2], ident[:])
                 if q >= vector_from:
-                    nc.vector.tensor_copy(out=dst(q), in_=bank[:].rearrange("p g u r -> p g r u"))
+                    nc.vector.tensor_copy(out=dst(q), in_=bank[:])
                 else:
-                    nc.scalar.copy(out=dst(q), in_=bank[:].rearrange("p g u r -> p g r u"))
+                    nc.scalar.copy(out=dst(q), in_=bank[:])
 
         def evac(t, vector_from=W // 2):
             grouped[t] = stage.tile([P, W * K], BF16, name="grouped", bufs=2, align_bytes=64)

@@ -162,8 +162,8 @@ def tile_dendriticlayersilu_ffn_kernel(tc, x, template_flat_bytes, template_flat
                     nc.vector.tensor_tensor(out=d[t][:, w, :], in0=bank[:], in1=run[t][:], op=ALU.subtract)
                 units(between[i])
 
-        def exp_pass(t):
-            for c in range(2):
+        def exp_pass(t, halves):
+            for c in halves:
                 cs = slice(c * 256, (c + 1) * 256)
                 nc.scalar.activation(out=d[t][:, :, cs], in_=d[t][:, :, cs], func=ACT.Exp)
 
@@ -282,7 +282,7 @@ def tile_dendriticlayersilu_ffn_kernel(tc, x, template_flat_bytes, template_flat
                     widen(t)
             for i in range(BATCH):
                 if b + 1 < NB:
-                    evac(batches[b + 1][i], vector_from=(0 if b + 2 >= NB else W // 2 - i))
+                    evac(batches[b + 1][i], vector_from=(0 if b + 2 >= NB else W // 2))
                 units([("d", t0 - 1, 2 * i), ("d", t0 - 1, 2 * i + 1)])
             units([("n", t0 - 1, nb) for nb in range(NT)])
             if b + 1 < NB:
@@ -293,11 +293,12 @@ def tile_dendriticlayersilu_ffn_kernel(tc, x, template_flat_bytes, template_flat
                 finish(t0 - 1)
             elif b >= 1:
                 log_pass([t0 - 1])
+                exp_pass(cur[0], [0])
                 recip_pass(batches[b - 1])
                 for t in batches[b - 1]:
                     finish(t)
-            for t in cur:
-                exp_pass(t)
+            exp_pass(cur[0], [1] if 1 <= b < NB - 1 else [0, 1])
+            exp_pass(cur[1], [0, 1])
             if b + 1 < NB:
                 nc.gpsimd.tensor_copy(out=seen_by_gpsimd[:], in_=t_codes[t0 + 3][:, W * P - 1 : W * P])
                 for t in cur:

@@ -127,11 +127,12 @@ def tile_dendriticlayersilu_ffn_kernel(tc, x, template_flat_bytes, template_flat
                         acc_n[t] = psum.tile([P, N], F32, name="acc", bufs=3)
                     window_sum(acc_n[t], f[t], nb)
 
-        def max_pass(tiles, between):
-            for t in tiles:
-                run[t] = small.tile([P, N], F32, name="run", bufs=4)
+        def max_pass(tiles, between, bursts):
             order = [(t, w) for w in range(W) for t in tiles]
-            for i in range(len(order) // BURST):
+            for i in bursts:
+                if i == 0:
+                    for t in tiles:
+                        run[t] = small.tile([P, N], F32, name="run", bufs=4)
                 part = order[i * BURST : (i + 1) * BURST]
                 banks = []
                 for t, w in part:
@@ -251,7 +252,7 @@ def tile_dendriticlayersilu_ffn_kernel(tc, x, template_flat_bytes, template_flat
         nc.gpsimd.tensor_copy(out=seen_by_gpsimd[:], in_=x_codes[:, W * N - 1 : W * N])
         scale_on_gpsimd(2)
         scale_on_gpsimd(3)
-        max_pass(batches[0], [[], [], [], []])
+        max_pass(batches[0], [[], [], [], []], [0, 1, 2, 3])
 
         for b in range(NB):
             cur = batches[b]
@@ -295,8 +296,6 @@ def tile_dendriticlayersilu_ffn_kernel(tc, x, template_flat_bytes, template_flat
                 log_pass([t0 - 1])
                 exp_pass(cur[0], [0])
                 recip_pass(batches[b - 1])
-                for t in batches[b - 1]:
-                    finish(t)
             exp_pass(cur[0], [1] if 1 <= b < NB - 1 else [0, 1])
             exp_pass(cur[1], [0, 1])
             if b + 1 < NB:
@@ -305,15 +304,17 @@ def tile_dendriticlayersilu_ffn_kernel(tc, x, template_flat_bytes, template_flat
                     for nb in range(NT):
                         bs = slice(nb * P, (nb + 1) * P)
                         nc.gpsimd.tensor_tensor(out=f[t][:, :, bs], in0=f[t][:, :, bs], in1=d[t][:, :, bs], op=ALU.mult)
-                max_pass(
-                    batches[b + 1],
-                    [
-                        [],
-                        [("d", t0, 0), ("d", t0, 1)],
-                        [("d", t0, 2), ("d", t0, 3)],
-                        [("n", t0, 0), ("n", t0, 1)],
-                    ],
-                )
+                sums_in_max_pass = [
+                    [],
+                    [("d", t0, 0), ("d", t0, 1)],
+                    [("d", t0, 2), ("d", t0, 3)],
+                    [("n", t0, 0), ("n", t0, 1)],
+                ]
+                max_pass(batches[b + 1], sums_in_max_pass, [0, 1])
+                if b >= 1:
+                    for t in batches[b - 1]:
+                        finish(t)
+                max_pass(batches[b + 1], sums_in_max_pass, [2, 3])
             else:
                 units([("d", cur[0], nb) for nb in range(NT)])
                 for t in cur:

@@ -134,16 +134,15 @@ def tile_dendriticlayersilu_ffn_kernel(tc, x, template_flat_bytes, template_flat
                     for t in tiles:
                         run[t] = small.tile([P, N], F32, name="run", bufs=4)
                 part = order[i * BURST : (i + 1) * BURST]
-                banks = []
+                banks = {}
+                for t, w in sorted(part):
+                    banks[(t, w)] = psum.tile([P, N], F32, name="rot")
+                    scores(banks[(t, w)], t, w)
                 for t, w in part:
-                    bank = psum.tile([P, N], F32, name="rot")
-                    scores(bank, t, w)
-                    banks.append(bank)
-                for (t, w), bank in zip(part, banks):
                     if w == 0:
-                        nc.vector.tensor_copy(out=run[t][:], in_=bank[:])
+                        nc.vector.tensor_copy(out=run[t][:], in_=banks[(t, w)][:])
                     else:
-                        nc.vector.tensor_tensor(out=run[t][:], in0=bank[:], in1=run[t][:], op=ALU.max)
+                        nc.vector.tensor_tensor(out=run[t][:], in0=banks[(t, w)][:], in1=run[t][:], op=ALU.max)
                 units(between[i])
 
         def sub_silu(tiles, between):
@@ -159,8 +158,8 @@ def tile_dendriticlayersilu_ffn_kernel(tc, x, template_flat_bytes, template_flat
                     scores(bank, t, w)
                     banks.append(bank)
                 for (t, w), bank in zip(part, banks):
-                    nc.scalar.activation(out=f[t][:, w, :], in_=bank[:], func=ACT.Silu)
                     nc.vector.tensor_tensor(out=d[t][:, w, :], in0=bank[:], in1=run[t][:], op=ALU.subtract)
+                    nc.scalar.activation(out=f[t][:, w, :], in_=bank[:], func=ACT.Silu)
                 units(between[i])
 
         def exp_pass(t, halves):

@@ -162,10 +162,9 @@ def tile_dendriticlayersilu_ffn_kernel(tc, x, template_flat_bytes, template_flat
                     nc.scalar.activation(out=f[t][:, w, :], in_=bank[:], func=ACT.Silu)
                 units(between[i])
 
-        def exp_pass(t, halves):
-            for c in halves:
-                cs = slice(c * 256, (c + 1) * 256)
-                nc.scalar.activation(out=d[t][:, :, cs], in_=d[t][:, :, cs], func=ACT.Exp)
+        def exp_pass(t, cuts):
+            for lo, hi in zip(cuts[:-1], cuts[1:]):
+                nc.scalar.activation(out=d[t][:, :, lo:hi], in_=d[t][:, :, lo:hi], func=ACT.Exp)
 
         def window_sum(acc, src, nb):
             bs = slice(nb * P, (nb + 1) * P)
@@ -293,10 +292,10 @@ def tile_dendriticlayersilu_ffn_kernel(tc, x, template_flat_bytes, template_flat
                 finish(t0 - 1)
             elif b >= 1:
                 log_pass([t0 - 1])
-                exp_pass(cur[0], [0])
+                exp_pass(cur[0], [0, 128])
                 recip_pass(batches[b - 1])
-            exp_pass(cur[0], [1] if 1 <= b < NB - 1 else [0, 1])
-            exp_pass(cur[1], [0, 1])
+            exp_pass(cur[0], [128, 256, 512] if 1 <= b < NB - 1 else [0, 128, 256, 512])
+            exp_pass(cur[1], [0, 256, 512])
             if b + 1 < NB:
                 nc.gpsimd.tensor_copy(out=seen_by_gpsimd[:], in_=t_codes[t0 + 3][:, W * P - 1 : W * P])
                 for t in cur:

@@ -59,6 +59,7 @@ def tile_dendriticlayersilu_ffn_kernel(tc, x, template_flat_bytes, template_flat
         acc_n = {}
         ln_d = {}
         r_d = {}
+        bank_of = {}
 
         def load_bytes(t):
             tb[t] = stage.tile([P, W * K], U8, name="tb", bufs=4)
@@ -127,40 +128,49 @@ def tile_dendriticlayersilu_ffn_kernel(tc, x, template_flat_bytes, template_flat
                         acc_n[t] = psum.tile([P, N], F32, name="acc", bufs=3)
                     window_sum(acc_n[t], f[t], nb)
 
-        def max_pass(tiles, between, bursts):
-            order = [(t, w) for w in range(W) for t in tiles]
-            for i in bursts:
-                if i == 0:
-                    for t in tiles:
-                        run[t] = small.tile([P, N], F32, name="run", bufs=4)
-                part = order[i * BURST : (i + 1) * BURST]
-                banks = {}
-                for t, w in sorted(part):
-                    banks[(t, w)] = psum.tile([P, N], F32, name="rot")
-                    scores(banks[(t, w)], t, w)
-                for t, w in part:
-                    if w == 0:
-                        nc.vector.tensor_copy(out=run[t][:], in_=banks[(t, w)][:])
-                    else:
-                        nc.vector.tensor_tensor(out=run[t][:], in0=banks[(t, w)][:], in1=run[t][:], op=ALU.max)
+        def issue(keys):
+            for key in keys:
+                bank_of[key] = psum.tile([P, N], F32, name="rot")
+                scores(bank_of[key], key[1], key[2])
+
+        def score_pass(name, reads, queue, read, between, after_second):
+            ahead = BURST + 1 - sum(1 for t, w in reads if (name, t, w) in bank_of)
+            issue(queue[:ahead])
+            rest = queue[ahead:]
+            for i in range(len(reads) // BURST):
+                for t, w in reads[i * BURST : (i + 1) * BURST]:
+                    read(t, w, bank_of[(name, t, w)])
+                if i == 1:
+                    for t in after_second:
+                        finish(t)
                 units(between[i])
+                issue(rest[i * BURST : (i + 1) * BURST])
+
+        def read_max(t, w, bank):
+            if w == 0:
+                run[t] = small.tile([P, N], F32, name="run", bufs=4)
+                nc.vector.tensor_copy(out=run[t][:], in_=bank[:])
+            else:
+                nc.vector.tensor_tensor(out=run[t][:], in0=bank[:], in1=run[t][:], op=ALU.max)
+
+        def read_sub_silu(t, w, bank):
+            if w == 0:
+                f[t] = work.tile([P, W, N], F32, name="f", align_bytes=64)
+                d[t] = work.tile([P, W, N], F32, name="d", align_bytes=64)
+            nc.vector.tensor_tensor(out=d[t][:, w, :], in0=bank[:], in1=run[t][:], op=ALU.subtract)
+            nc.scalar.activation(out=f[t][:, w, :], in_=bank[:], func=ACT.Silu)
+
+        def max_pass(tiles, between, after_second):
+            reads = [(t, w) for w in range(W) for t in tiles]
+            queue = []
+            for i in range(len(reads) // BURST):
+                queue.extend(("max", t, w) for t, w in sorted(reads[i * BURST : (i + 1) * BURST]))
+            queue.append(("sub", tiles[0], 0))
+            score_pass("max", reads, queue, read_max, between, after_second)
 
         def sub_silu(tiles, between):
-            order = [(t, w) for t in tiles for w in range(W)]
-            for i in range(len(order) // BURST):
-                part = order[i * BURST : (i + 1) * BURST]
-                banks = []
-                for t, w in part:
-                    if w == 0:
-                        f[t] = work.tile([P, W, N], F32, name="f", align_bytes=64)
-                        d[t] = work.tile([P, W, N], F32, name="d", align_bytes=64)
-                    bank = psum.tile([P, N], F32, name="rot")
-                    scores(bank, t, w)
-                    banks.append(bank)
-                for (t, w), bank in zip(part, banks):
-                    nc.vector.tensor_tensor(out=d[t][:, w, :], in0=bank[:], in1=run[t][:], op=ALU.subtract)
-                    nc.scalar.activation(out=f[t][:, w, :], in_=bank[:], func=ACT.Silu)
-                units(between[i])
+            reads = [(t, w) for t in tiles for w in range(W)]
+            score_pass("sub", reads, [("sub", t, w) for t, w in reads[1:]], read_sub_silu, between, [])
 
         def exp_pass(t, cuts):
             for lo, hi in zip(cuts[:-1], cuts[1:]):
@@ -250,7 +260,7 @@ def tile_dendriticlayersilu_ffn_kernel(tc, x, template_flat_bytes, template_flat
         nc.gpsimd.tensor_copy(out=seen_by_gpsimd[:], in_=x_codes[:, W * N - 1 : W * N])
         scale_on_gpsimd(2)
         scale_on_gpsimd(3)
-        max_pass(batches[0], [[], [], [], []], [0, 1, 2, 3])
+        max_pass(batches[0], [[], [], [], []], [])
 
         for b in range(NB):
             cur = batches[b]
@@ -308,11 +318,7 @@ def tile_dendriticlayersilu_ffn_kernel(tc, x, template_flat_bytes, template_flat
                     [("d", t0, 2), ("d", t0, 3)],
                     [("n", t0, 0), ("n", t0, 1)],
                 ]
-                max_pass(batches[b + 1], sums_in_max_pass, [0, 1])
-                if b >= 1:
-                    for t in batches[b - 1]:
-                        finish(t)
-                max_pass(batches[b + 1], sums_in_max_pass, [2, 3])
+                max_pass(batches[b + 1], sums_in_max_pass, batches[b - 1] if b >= 1 else [])
             else:
                 units([("d", cur[0], nb) for nb in range(NT)])
                 for t in cur:

@@ -308,10 +308,9 @@ def tile_dendriticlayersilu_ffn_kernel(tc, x, template_flat_bytes, template_flat
             exp_pass(cur[1], [0, 256, 512])
             if b + 1 < NB:
                 nc.gpsimd.tensor_copy(out=seen_by_gpsimd[:], in_=t_codes[t0 + 3][:, W * P - 1 : W * P])
-                for t in cur:
-                    for nb in range(NT):
-                        bs = slice(nb * P, (nb + 1) * P)
-                        nc.gpsimd.tensor_tensor(out=f[t][:, :, bs], in0=f[t][:, :, bs], in1=d[t][:, :, bs], op=ALU.mult)
+                for t, cuts in ((cur[0], [0, 128, 256, 512]), (cur[1], [0, 256, 512])):
+                    for lo, hi in zip(cuts[:-1], cuts[1:]):
+                        nc.gpsimd.tensor_tensor(out=f[t][:, :, lo:hi], in0=f[t][:, :, lo:hi], in1=d[t][:, :, lo:hi], op=ALU.mult)
                 sums_in_max_pass = [
                     [],
                     [("d", t0, 0), ("d", t0, 1)],

@@ -65,10 +65,10 @@ def tile_dendriticlayersilu_ffn_kernel(tc, x, template_flat_bytes, template_flat
             tb[t] = stage.tile([P, W * K], U8, name="tb", bufs=4)
             nc.sync.dma_start(out=tb[t][:], in_=template_flat_bytes[t * P : (t + 1) * P, :])
 
-        def widen(t):
+        def widen(t, cuts=(0, 2048, 4096)):
             wb[t] = stage.tile([P, W * K], BF16, name="wb", bufs=3)
-            for c in range(2):
-                cs = slice(c * 2048, (c + 1) * 2048)
+            for lo, hi in zip(cuts[:-1], cuts[1:]):
+                cs = slice(lo, hi)
                 nc.vector.tensor_tensor(
                     out=wb[t][:, cs], in0=tb[t][:, cs].bitcast(FP8), in1=scale_bc[:, cs], op=ALU.mult
                 )
@@ -214,23 +214,36 @@ def tile_dendriticlayersilu_ffn_kernel(tc, x, template_flat_bytes, template_flat
             nc.sync.dma_start(out=xc[:], in_=x_view[:, :, a * 4 * K : (a + 1) * 4 * K])
             x_cols.append(xc)
 
+        sc_rows = keep.tile([P, P], F32, name="sc_rows")
+        nc.vector.memset(sc_rows[:], 0.0)
+        nc.sync.dma_start(out=sc_rows[0 : W * K // P, :], in_=template_flat_scale.rearrange("o (c k) -> (o c) k", k=P))
         load_bytes(0)
-        for c in range(2):
-            cs = slice(c * 2048, (c + 1) * 2048)
-            nc.sync.dma_start(
-                out=scale_bc[:, cs], in_=template_flat_scale[:, cs].rearrange("o k -> (o k)").partition_broadcast(P)
-            )
         load_bytes(1)
         load_x(0)
+        load_x(1)
         load_bytes(2)
         load_bytes(3)
-        load_x(1)
-        widen(0)
+        sc_turned = psum.tile([P, P], F32, name="rot")
+        nc.tensor.transpose(sc_turned[:], sc_rows[:], ident[:])
+        sc_cols = keep.tile([P, W * K // P], F32, name="sc_cols")
+        nc.scalar.copy(out=sc_cols[:], in_=sc_turned[:, 0 : W * K // P])
+        for g in range(W):
+            bank = psum.tile([P, K], F32, name="rot")
+            for q in range(K // P):
+                c = g * (K // P) + q
+                nc.tensor.matmul(
+                    out=bank[:, q * P : (q + 1) * P],
+                    lhsT=sc_cols[:, c : c + 1].to_broadcast([P, P]),
+                    rhs=ident[:],
+                    is_transpose=True,
+                    start=True,
+                    stop=True,
+                )
+            nc.scalar.copy(out=scale_bc[:, g * K : (g + 1) * K], in_=bank[:])
+        widen(0, tuple(range(0, W * K + 1, K)))
         widen(1)
         load_bytes(4)
         load_bytes(5)
-        cast(2)
-        cast(3)
         x_grouped = []
         xg_words = []
         for a in range(2):
@@ -253,10 +266,14 @@ def tile_dendriticlayersilu_ffn_kernel(tc, x, template_flat_bytes, template_flat
                     in_=x_grouped[a][:, c * 4096 : (c + 1) * 4096],
                 )
 
-        for a in range(2):
-            evac(a)
-            quant(a)
-            prepare_x(a)
+        evac(0)
+        quant(0)
+        prepare_x(0)
+        evac(1)
+        quant(1)
+        cast(2)
+        cast(3)
+        prepare_x(1)
         nc.gpsimd.tensor_copy(out=seen_by_gpsimd[:], in_=x_codes[:, W * N - 1 : W * N])
         scale_on_gpsimd(2)
         scale_on_gpsimd(3)

@@ -149,7 +149,10 @@ def tile_dendriticlayersilu_ffn_kernel(tc, x, template_flat_bytes, template_flat
         def read_max(t, w, bank):
             if w == 0:
                 run[t] = small.tile([P, N], F32, name="run", bufs=4)
-                nc.vector.tensor_copy(out=run[t][:], in_=bank[:])
+                if t < BATCH:
+                    nc.scalar.copy(out=run[t][:], in_=bank[:])
+                else:
+                    nc.vector.tensor_copy(out=run[t][:], in_=bank[:])
             else:
                 nc.vector.tensor_tensor(out=run[t][:], in0=bank[:], in1=run[t][:], op=ALU.max)
 
@@ -305,7 +308,7 @@ def tile_dendriticlayersilu_ffn_kernel(tc, x, template_flat_bytes, template_flat
                 else:
                     nc.vector.tensor_copy(out=seen_by_vector[:], in_=wb[3][:, W * K - 1 : W * K])
                 for t in batches[b + 2]:
-                    widen(t)
+                    widen(t, (0, W * K))
             for i in range(BATCH):
                 if b + 1 < NB:
                     evac(batches[b + 1][i], vector_from=(0 if b + 2 >= NB else W // 2))

@@ -212,18 +212,22 @@ def tile_dendriticlayersilu_ffn_kernel(tc, x, template_flat_bytes, template_flat
 
         x_cols = []
 
-        def load_x(a):
-            xc = work.tile([P, NT, 4 * K], BF16, name="d", align_bytes=64)
-            nc.sync.dma_start(out=xc[:], in_=x_view[:, :, a * 4 * K : (a + 1) * 4 * K])
-            x_cols.append(xc)
+        def load_x(a, c):
+            if c == 0:
+                x_cols.append(work.tile([P, NT, 4 * K], BF16, name="d", align_bytes=64))
+            nc.sync.dma_start(
+                out=x_cols[a][:, :, c * 2 * K : (c + 1) * 2 * K], in_=x_view[:, :, (2 * a + c) * 2 * K : (2 * a + c + 1) * 2 * K]
+            )
 
         sc_rows = keep.tile([P, P], F32, name="sc_rows")
         nc.vector.memset(sc_rows[:], 0.0)
         nc.sync.dma_start(out=sc_rows[0 : W * K // P, :], in_=template_flat_scale.rearrange("o (c k) -> (o c) k", k=P))
         load_bytes(0)
+        load_x(0, 0)
         load_bytes(1)
-        load_x(0)
-        load_x(1)
+        load_x(0, 1)
+        load_x(1, 0)
+        load_x(1, 1)
         load_bytes(2)
         load_bytes(3)
         sc_turned = psum.tile([P, P], F32, name="rot")
@@ -255,13 +259,13 @@ def tile_dendriticlayersilu_ffn_kernel(tc, x, template_flat_bytes, template_flat
             xg_words.append(xg[:].bitcast(F32).rearrange("p (g n u) -> p g n u", g=4, u=2))
 
         def prepare_x(a):
-            for i in range(NT):
-                turn(
-                    x_cols[a][:, i, :].bitcast(F32),
-                    lambda q: xg_words[a][:, 2 * q : 2 * q + 2, i * P : (i + 1) * P, :],
-                    banks=2,
-                )
             for c in range(2):
+                for i in range(NT):
+                    turn(
+                        x_cols[a][:, i, c * 2 * K : (c + 1) * 2 * K].bitcast(F32),
+                        lambda q: xg_words[a][:, 2 * c : 2 * c + 2, i * P : (i + 1) * P, :],
+                        banks=1,
+                    )
                 g = 4 * a + 2 * c
                 nc.vector.quantize_mx(
                     out=x_codes[:, g * N : (g + 2) * N].bitcast(FP8X4),

@@ -221,6 +221,8 @@ def tile_dendriticlayersilu_ffn_kernel(tc, x, template_flat_bytes, template_flat
 
         sc_rows = keep.tile([P, P], F32, name="sc_rows")
         nc.vector.memset(sc_rows[:], 0.0)
+        clock_work = keep.tile([P, N], BF16, name="clock_work")
+        nc.vector.memset(clock_work[:], 0.0)
         nc.sync.dma_start(out=sc_rows[0 : W * K // P, :], in_=template_flat_scale.rearrange("o (c k) -> (o c) k", k=P))
         load_bytes(0)
         load_x(0, 0)
@@ -230,6 +232,9 @@ def tile_dendriticlayersilu_ffn_kernel(tc, x, template_flat_bytes, template_flat
         load_x(1, 1)
         load_bytes(2)
         load_bytes(3)
+        unread = psum.tile([P, N], F32, name="rot")
+        for i in range(5):
+            nc.tensor.matmul(out=unread[:], lhsT=clock_work[:, 0:P], rhs=clock_work[:], start=True, stop=True)
         sc_turned = psum.tile([P, P], F32, name="rot")
         nc.tensor.transpose(sc_turned[:], sc_rows[:], ident[:])
         sc_cols = keep.tile([P, W * K // P], F32, name="sc_cols")

@@ -24,6 +24,7 @@ NT = N // P
 BATCH = 2
 BURST = 4
 NB = HT // BATCH
+G_SHARE = 1024
 
 
 def tile_dendriticlayersilu_ffn_kernel(tc, x, template_flat_bytes, template_flat_scale, out):
@@ -40,7 +41,7 @@ def tile_dendriticlayersilu_ffn_kernel(tc, x, template_flat_bytes, template_flat
         make_identity(nc, ident[:])
         x_codes = keep.tile([P, W * N], U32, name="x_codes", align_bytes=64)
         x_scales = keep.tile([P, W * N], U8, name="x_scales", align_bytes=64)
-        scale_bc = keep.tile([P, W * K], F32, name="scale_bc")
+        scales4 = keep.tile([P, W, 4], F32, name="scales4")
         seen_by_vector = keep.tile([P, 1], F32, name="seen_by_vector")
         seen_by_gpsimd = keep.tile([P, 1], U32, name="seen_by_gpsimd")
 
@@ -65,22 +66,15 @@ def tile_dendriticlayersilu_ffn_kernel(tc, x, template_flat_bytes, template_flat
             tb[t] = stage.tile([P, W * K], U8, name="tb", bufs=4)
             nc.sync.dma_start(out=tb[t][:], in_=template_flat_bytes[t * P : (t + 1) * P, :])
 
-        def widen(t, cuts=(0, 2048, 4096)):
-            wb[t] = stage.tile([P, W * K], BF16, name="wb", bufs=3)
-            for lo, hi in zip(cuts[:-1], cuts[1:]):
-                cs = slice(lo, hi)
-                nc.vector.tensor_tensor(
-                    out=wb[t][:, cs], in0=tb[t][:, cs].bitcast(FP8), in1=scale_bc[:, cs], op=ALU.mult
-                )
-
-        def cast(t):
-            wb[t] = stage.tile([P, W * K], BF16, name="wb", bufs=3)
-            nc.vector.tensor_copy(out=wb[t][:], in_=tb[t][:].bitcast(FP8))
-
-        def scale_on_gpsimd(t):
-            for c in range(2):
-                cs = slice(c * 2048, (c + 1) * 2048)
-                nc.gpsimd.tensor_tensor(out=wb[t][:, cs], in0=wb[t][:, cs], in1=scale_bc[:, cs], op=ALU.mult)
+        def cast(t, shares):
+            wb[t] = stage.tile([P, W * K], BF16, name="wb", bufs=4)
+            for who, lo, hi in shares:
+                if who == "g":
+                    nc.gpsimd.tensor_copy(out=wb[t][:, lo:hi], in_=tb[t][:, lo:hi].bitcast(FP8))
+                elif who == "s":
+                    nc.scalar.copy(out=wb[t][:, lo:hi], in_=tb[t][:, lo:hi].bitcast(FP8))
+                else:
+                    nc.vector.tensor_copy(out=wb[t][:, lo:hi], in_=tb[t][:, lo:hi].bitcast(FP8))
 
         def turn(words, dst, banks=W // 2, vector_from=W // 2):
             for q in range(banks):
@@ -94,10 +88,22 @@ def tile_dendriticlayersilu_ffn_kernel(tc, x, template_flat_bytes, template_flat
                 else:
                     nc.scalar.copy(out=dst(q), in_=bank[:])
 
-        def evac(t, vector_from=W // 2):
+        def evac(t):
             grouped[t] = stage.tile([P, W * K], BF16, name="grouped", bufs=2, align_bytes=64)
-            g_words = grouped[t][:].bitcast(F32).rearrange("p (g r u) -> p g r u", g=W, u=2)
-            turn(wb[t][:].bitcast(F32), lambda q: g_words[:, 2 * q : 2 * q + 2, :, :], vector_from=vector_from)
+            g_vals = grouped[t][:].rearrange("p (g r e) -> p g r e", g=W, e=4)
+            words = wb[t][:].bitcast(F32)
+            for q in range(W // 2):
+                bank = psum.tile([P, 2, P, 2], F32, name="rot")
+                for gg in range(2):
+                    g = 2 * q + gg
+                    for u in range(2):
+                        nc.tensor.transpose(bank[:, gg, :, u], words[:, 256 * g + u : 256 * (g + 1) : 2], ident[:])
+                nc.vector.tensor_tensor(
+                    out=g_vals[:, 2 * q : 2 * q + 2, :, :],
+                    in0=bank[:].rearrange("p g r u -> p (g r u)").bitcast(BF16).rearrange("p (g r e) -> p g r e", g=2, e=4),
+                    in1=scales4[:, 2 * q : 2 * q + 2, :].unsqueeze(2).to_broadcast([P, 2, P, 4]),
+                    op=ALU.mult,
+                )
 
         def quant(t):
             t_codes[t] = stage.tile([P, W * P], U32, name="t_codes", bufs=4, align_bytes=64)
@@ -133,26 +139,23 @@ def tile_dendriticlayersilu_ffn_kernel(tc, x, template_flat_bytes, template_flat
                 bank_of[key] = psum.tile([P, N], F32, name="rot")
                 scores(bank_of[key], key[1], key[2])
 
-        def score_pass(name, reads, queue, read, between, after_second):
+        def score_pass(name, reads, queue, read, between, before):
             ahead = BURST + 1 - sum(1 for t, w in reads if (name, t, w) in bank_of)
             issue(queue[:ahead])
             rest = queue[ahead:]
+            for t in before:
+                finish(t)
             for i in range(len(reads) // BURST):
                 for t, w in reads[i * BURST : (i + 1) * BURST]:
                     read(t, w, bank_of[(name, t, w)])
-                if i == 1:
-                    for t in after_second:
-                        finish(t)
                 units(between[i])
                 issue(rest[i * BURST : (i + 1) * BURST])
 
         def read_max(t, w, bank):
             if w == 0:
-                run[t] = small.tile([P, N], F32, name="run", bufs=4)
-                if t < BATCH:
+                if t not in run:
+                    run[t] = small.tile([P, N], F32, name="run", bufs=4)
                     nc.scalar.copy(out=run[t][:], in_=bank[:])
-                else:
-                    nc.vector.tensor_copy(out=run[t][:], in_=bank[:])
             else:
                 nc.vector.tensor_tensor(out=run[t][:], in0=bank[:], in1=run[t][:], op=ALU.max)
 
@@ -163,13 +166,24 @@ def tile_dendriticlayersilu_ffn_kernel(tc, x, template_flat_bytes, template_flat
             nc.vector.tensor_tensor(out=d[t][:, w, :], in0=bank[:], in1=run[t][:], op=ALU.subtract)
             nc.scalar.activation(out=f[t][:, w, :], in_=bank[:], func=ACT.Silu)
 
-        def max_pass(tiles, between, after_second):
+        def max_plan(tiles):
             reads = [(t, w) for w in range(W) for t in tiles]
             queue = []
             for i in range(len(reads) // BURST):
                 queue.extend(("max", t, w) for t, w in sorted(reads[i * BURST : (i + 1) * BURST]))
             queue.append(("sub", tiles[0], 0))
-            score_pass("max", reads, queue, read_max, between, after_second)
+            return reads, queue
+
+        def max_start(tiles):
+            reads, queue = max_plan(tiles)
+            issue(queue[: BURST + 1])
+            for t in tiles:
+                read_max(t, 0, bank_of[("max", t, 0)])
+
+        def max_pass(tiles, between, before):
+            reads, queue = max_plan(tiles)
+            started = sum(1 for key in queue if key in bank_of)
+            score_pass("max", reads, queue[started:], read_max, between, before)
 
         def sub_silu(tiles, between):
             reads = [(t, w) for t in tiles for w in range(W)]
@@ -219,11 +233,9 @@ def tile_dendriticlayersilu_ffn_kernel(tc, x, template_flat_bytes, template_flat
                 out=x_cols[a][:, :, c * 2 * K : (c + 1) * 2 * K], in_=x_view[:, :, (2 * a + c) * 2 * K : (2 * a + c + 1) * 2 * K]
             )
 
-        sc_rows = keep.tile([P, P], F32, name="sc_rows")
-        nc.vector.memset(sc_rows[:], 0.0)
         clock_work = keep.tile([P, N], BF16, name="clock_work")
         nc.vector.memset(clock_work[:], 0.0)
-        nc.sync.dma_start(out=sc_rows[0 : W * K // P, :], in_=template_flat_scale.rearrange("o (c k) -> (o c) k", k=P))
+        nc.sync.dma_start(out=scales4[:], in_=template_flat_scale.rearrange("o (g p e) -> p (o g) e", p=P, e=4))
         load_bytes(0)
         load_x(0, 0)
         load_bytes(1)
@@ -235,25 +247,8 @@ def tile_dendriticlayersilu_ffn_kernel(tc, x, template_flat_bytes, template_flat
         unread = psum.tile([P, N], F32, name="rot")
         for i in range(5):
             nc.tensor.matmul(out=unread[:], lhsT=clock_work[:, 0:P], rhs=clock_work[:], start=True, stop=True)
-        sc_turned = psum.tile([P, P], F32, name="rot")
-        nc.tensor.transpose(sc_turned[:], sc_rows[:], ident[:])
-        sc_cols = keep.tile([P, W * K // P], F32, name="sc_cols")
-        nc.scalar.copy(out=sc_cols[:], in_=sc_turned[:, 0 : W * K // P])
-        for g in range(W):
-            bank = psum.tile([P, K], F32, name="rot")
-            for q in range(K // P):
-                c = g * (K // P) + q
-                nc.tensor.matmul(
-                    out=bank[:, q * P : (q + 1) * P],
-                    lhsT=sc_cols[:, c : c + 1].to_broadcast([P, P]),
-                    rhs=ident[:],
-                    is_transpose=True,
-                    start=True,
-                    stop=True,
-                )
-            nc.scalar.copy(out=scale_bc[:, g * K : (g + 1) * K], in_=bank[:])
-        widen(0, tuple(range(0, W * K + 1, K)))
-        widen(1)
+        cast(0, [("s", 0, 1024), ("g", 2048, 3072), ("s", 1024, 2048), ("g", 3072, 4096)])
+        cast(1, [("s", 0, 1024), ("g", 2048, 3072), ("s", 1024, 2048), ("g", 3072, 4096)])
         load_bytes(4)
         load_bytes(5)
         x_grouped = []
@@ -279,16 +274,14 @@ def tile_dendriticlayersilu_ffn_kernel(tc, x, template_flat_bytes, template_flat
                 )
 
         evac(0)
-        quant(0)
-        prepare_x(0)
         evac(1)
+        quant(0)
         quant(1)
-        cast(2)
-        cast(3)
+        prepare_x(0)
         prepare_x(1)
         nc.gpsimd.tensor_copy(out=seen_by_gpsimd[:], in_=x_codes[:, W * N - 1 : W * N])
-        scale_on_gpsimd(2)
-        scale_on_gpsimd(3)
+        cast(2, [("g", 0, W * K)])
+        cast(3, [("g", 0, W * K)])
         max_pass(batches[0], [[], [], [], []], [])
 
         for b in range(NB):
@@ -312,18 +305,16 @@ def tile_dendriticlayersilu_ffn_kernel(tc, x, template_flat_bytes, template_flat
             elif b >= 1:
                 log_pass([t0 - 2])
             if b + 2 < NB:
-                if b >= 1:
-                    nc.vector.tensor_copy(out=seen_by_vector[:], in_=f[t0 - 1][:, W - 1, N - 1 : N])
-                else:
-                    nc.vector.tensor_copy(out=seen_by_vector[:], in_=wb[3][:, W * K - 1 : W * K])
-                for t in batches[b + 2]:
-                    widen(t, (0, W * K))
+                cast(batches[b + 2][0], [("g", 0, W * K)])
+                cast(batches[b + 2][1], [("g", 0, G_SHARE), ("s", G_SHARE, W * K)])
             for i in range(BATCH):
                 if b + 1 < NB:
-                    evac(batches[b + 1][i], vector_from=(0 if b + 2 >= NB else W // 2))
+                    evac(batches[b + 1][i])
                 units([("d", t0 - 1, 2 * i), ("d", t0 - 1, 2 * i + 1)])
             units([("n", t0 - 1, nb) for nb in range(NT)])
             if b + 1 < NB:
+                if b + 2 < NB:
+                    nc.vector.tensor_copy(out=seen_by_vector[:], in_=wb[batches[b + 2][1]][:, G_SHARE - 1 : G_SHARE])
                 for t in batches[b + 1]:
                     quant(t)
             if b + 1 >= NB:
@@ -333,7 +324,11 @@ def tile_dendriticlayersilu_ffn_kernel(tc, x, template_flat_bytes, template_flat
                 log_pass([t0 - 1])
                 exp_pass(cur[0], [0, 128])
                 recip_pass(batches[b - 1])
-            exp_pass(cur[0], [128, 256, 512] if 1 <= b < NB - 1 else [0, 128, 256, 512])
+                max_start(batches[b + 1])
+            elif b == 0:
+                exp_pass(cur[0], [0, 128])
+                max_start(batches[b + 1])
+            exp_pass(cur[0], [128, 256, 512] if b < NB - 1 else [0, 128, 256, 512])
             exp_pass(cur[1], [0, 256, 512])
             if b + 1 < NB:
                 nc.gpsimd.tensor_copy(out=seen_by_gpsimd[:], in_=t_codes[t0 + 3][:, W * P - 1 : W * P])

@@ -24,7 +24,7 @@ NT = N // P
 BATCH = 2
 BURST = 4
 NB = HT // BATCH
-G_SHARE = 1024
+G_SHARE = 2560
 
 
 def tile_dendriticlayersilu_ffn_kernel(tc, x, template_flat_bytes, template_flat_scale, out):

@@ -67,7 +67,7 @@ def tile_dendriticlayersilu_ffn_kernel(tc, x, template_flat_bytes, template_flat
             nc.sync.dma_start(out=tb[t][:], in_=template_flat_bytes[t * P : (t + 1) * P, :])
 
         def cast(t, shares):
-            wb[t] = stage.tile([P, W * K], BF16, name="wb", bufs=4)
+            wb[t] = stage.tile([P, W * K], BF16, name="wb", bufs=3)
             for who, lo, hi in shares:
                 if who == "g":
                     nc.gpsimd.tensor_copy(out=wb[t][:, lo:hi], in_=tb[t][:, lo:hi].bitcast(FP8))
@@ -88,11 +88,12 @@ def tile_dendriticlayersilu_ffn_kernel(tc, x, template_flat_bytes, template_flat
                 else:
                     nc.scalar.copy(out=dst(q), in_=bank[:])
 
-        def evac(t):
-            grouped[t] = stage.tile([P, W * K], BF16, name="grouped", bufs=2, align_bytes=64)
+        def evac(t, banks):
+            if t not in grouped:
+                grouped[t] = stage.tile([P, W * K], BF16, name="grouped", bufs=2, align_bytes=64)
             g_vals = grouped[t][:].rearrange("p (g r e) -> p g r e", g=W, e=4)
             words = wb[t][:].bitcast(F32)
-            for q in range(W // 2):
+            for q in banks:
                 bank = psum.tile([P, 2, P, 2], F32, name="rot")
                 for gg in range(2):
                     g = 2 * q + gg
@@ -161,7 +162,7 @@ def tile_dendriticlayersilu_ffn_kernel(tc, x, template_flat_bytes, template_flat
 
         def read_sub_silu(t, w, bank):
             if w == 0:
-                f[t] = work.tile([P, W, N], F32, name="f", align_bytes=64)
+                f[t] = work.tile([P, W, N], F32, name="f", bufs=4, align_bytes=64)
                 d[t] = work.tile([P, W, N], F32, name="d", align_bytes=64)
             nc.vector.tensor_tensor(out=d[t][:, w, :], in0=bank[:], in1=run[t][:], op=ALU.subtract)
             nc.scalar.activation(out=f[t][:, w, :], in_=bank[:], func=ACT.Silu)
@@ -254,7 +255,7 @@ def tile_dendriticlayersilu_ffn_kernel(tc, x, template_flat_bytes, template_flat
         x_grouped = []
         xg_words = []
         for a in range(2):
-            xg = work.tile([P, 4 * N * 4], BF16, name="f", align_bytes=64)
+            xg = work.tile([P, 4 * N * 4], BF16, name="f", bufs=4, align_bytes=64)
             x_grouped.append(xg)
             xg_words.append(xg[:].bitcast(F32).rearrange("p (g n u) -> p g n u", g=4, u=2))
 
@@ -273,8 +274,8 @@ def tile_dendriticlayersilu_ffn_kernel(tc, x, template_flat_bytes, template_flat
                     in_=x_grouped[a][:, c * 4096 : (c + 1) * 4096],
                 )
 
-        evac(0)
-        evac(1)
+        evac(0, range(W // 2))
+        evac(1, range(W // 2))
         quant(0)
         quant(1)
         prepare_x(0)
@@ -292,12 +293,7 @@ def tile_dendriticlayersilu_ffn_kernel(tc, x, template_flat_bytes, template_flat
                     load_bytes(t)
             sub_silu(
                 cur,
-                [
-                    [("n", t0 - 2, 2)],
-                    [("n", t0 - 2, 3)],
-                    [],
-                    [],
-                ],
+                [[("n", t0 - 2, nb)] for nb in range(NT)],
             )
             if b + 1 >= NB:
                 divide(t0 - 2)
@@ -307,10 +303,12 @@ def tile_dendriticlayersilu_ffn_kernel(tc, x, template_flat_bytes, template_flat
             if b + 2 < NB:
                 cast(batches[b + 2][0], [("g", 0, W * K)])
                 cast(batches[b + 2][1], [("g", 0, G_SHARE), ("s", G_SHARE, W * K)])
-            for i in range(BATCH):
-                if b + 1 < NB:
-                    evac(batches[b + 1][i])
-                units([("d", t0 - 1, 2 * i), ("d", t0 - 1, 2 * i + 1)])
+            if b + 1 < NB:
+                evac(batches[b + 1][0], range(W // 2))
+                evac(batches[b + 1][1], [0])
+            units([("d", t0 - 1, nb) for nb in range(NT)])
+            if b + 1 < NB:
+                evac(batches[b + 1][1], range(1, W // 2))
             units([("n", t0 - 1, nb) for nb in range(NT)])
             if b + 1 < NB:
                 if b + 2 < NB:
@@ -324,23 +322,24 @@ def tile_dendriticlayersilu_ffn_kernel(tc, x, template_flat_bytes, template_flat
                 log_pass([t0 - 1])
                 exp_pass(cur[0], [0, 128])
                 recip_pass(batches[b - 1])
+                exp_pass(cur[0], [128, 256, 384])
                 max_start(batches[b + 1])
+                exp_pass(cur[0], [384, 512])
+                exp_pass(cur[1], [0, 256, 512])
             elif b == 0:
-                exp_pass(cur[0], [0, 128])
+                exp_pass(cur[0], [0, 128, 256, 512])
+                exp_pass(cur[1], [0, 256])
                 max_start(batches[b + 1])
-            exp_pass(cur[0], [128, 256, 512] if b < NB - 1 else [0, 128, 256, 512])
-            exp_pass(cur[1], [0, 256, 512])
+                exp_pass(cur[1], [256, 512])
+            if b + 1 >= NB:
+                exp_pass(cur[0], [0, 128, 256, 512])
+                exp_pass(cur[1], [0, 256, 512])
             if b + 1 < NB:
                 nc.gpsimd.tensor_copy(out=seen_by_gpsimd[:], in_=t_codes[t0 + 3][:, W * P - 1 : W * P])
                 for t, cuts in ((cur[0], [0, 128, 256, 512]), (cur[1], [0, 256, 512])):
                     for lo, hi in zip(cuts[:-1], cuts[1:]):
                         nc.gpsimd.tensor_tensor(out=f[t][:, :, lo:hi], in0=f[t][:, :, lo:hi], in1=d[t][:, :, lo:hi], op=ALU.mult)
-                sums_in_max_pass = [
-                    [],
-                    [("d", t0, 0), ("d", t0, 1)],
-                    [("d", t0, 2), ("d", t0, 3)],
-                    [("n", t0, 0), ("n", t0, 1)],
-                ]
+                sums_in_max_pass = [[("d", t0, nb)] for nb in range(NT)]
                 max_pass(batches[b + 1], sums_in_max_pass, batches[b - 1] if b >= 1 else [])
             else:
                 units([("d", cur[0], nb) for nb in range(NT)])

@@ -62,9 +62,12 @@ def tile_dendriticlayersilu_ffn_kernel(tc, x, template_flat_bytes, template_flat
         r_d = {}
         bank_of = {}
 
-        def load_bytes(t):
+        def load_bytes(t, pieces=1):
             tb[t] = stage.tile([P, W * K], U8, name="tb", bufs=4)
-            nc.sync.dma_start(out=tb[t][:], in_=template_flat_bytes[t * P : (t + 1) * P, :])
+            width = W * K // pieces
+            for i in range(pieces):
+                cs = slice(i * width, (i + 1) * width)
+                nc.sync.dma_start(out=tb[t][:, cs], in_=template_flat_bytes[t * P : (t + 1) * P, cs])
 
         def cast(t, shares):
             wb[t] = stage.tile([P, W * K], BF16, name="wb", bufs=3)
@@ -135,9 +138,12 @@ def tile_dendriticlayersilu_ffn_kernel(tc, x, template_flat_bytes, template_flat
                         acc_n[t] = psum.tile([P, N], F32, name="acc", bufs=3)
                     window_sum(acc_n[t], f[t], nb)
 
-        def issue(keys):
+        def issue(keys, lent=()):
             for key in keys:
-                bank_of[key] = psum.tile([P, N], F32, name="rot")
+                if key in lent:
+                    bank_of[key] = psum.tile([P, N], F32, name="acc", bufs=3)
+                else:
+                    bank_of[key] = psum.tile([P, N], F32, name="rot")
                 scores(bank_of[key], key[1], key[2])
 
         def score_pass(name, reads, queue, read, between, before):
@@ -168,23 +174,34 @@ def tile_dendriticlayersilu_ffn_kernel(tc, x, template_flat_bytes, template_flat
             nc.scalar.activation(out=f[t][:, w, :], in_=bank[:], func=ACT.Silu)
 
         def max_plan(tiles):
-            reads = [(t, w) for w in range(W) for t in tiles]
-            queue = []
-            for i in range(len(reads) // BURST):
-                queue.extend(("max", t, w) for t, w in sorted(reads[i * BURST : (i + 1) * BURST]))
-            queue.append(("sub", tiles[0], 0))
-            return reads, queue
+            first, second = tiles
+            reads = [(first, 0), (second, 0), (first, 1), (second, 1)]
+            queue = [("max", first, 0), ("max", first, 1), ("max", second, 0), ("max", second, 1)]
+            for w in range(2, W, 2):
+                reads.extend([(first, w + 1), (second, w + 1), (first, w), (second, w)])
+                queue.extend([("max", second, w), ("max", second, w + 1), ("max", first, w), ("max", first, w + 1)])
+            lent = [key for j, key in enumerate(queue) if j % 7 >= 5]
+            queue.append(("sub", first, 0))
+            return reads, queue, lent
 
         def max_start(tiles):
-            reads, queue = max_plan(tiles)
-            issue(queue[: BURST + 1])
+            reads, queue, lent = max_plan(tiles)
+            issue(queue[: BURST + 1], lent)
             for t in tiles:
                 read_max(t, 0, bank_of[("max", t, 0)])
 
         def max_pass(tiles, between, before):
-            reads, queue = max_plan(tiles)
+            reads, queue, lent = max_plan(tiles)
             started = sum(1 for key in queue if key in bank_of)
-            score_pass("max", reads, queue[started:], read_max, between, before)
+            issue(queue[started : 2 * BURST], lent)
+            rest = queue[2 * BURST :]
+            for t in before:
+                finish(t)
+            for i in range(len(reads) // BURST):
+                for t, w in reads[i * BURST : (i + 1) * BURST]:
+                    read_max(t, w, bank_of[("max", t, w)])
+                units(between[i])
+                issue(rest[i * BURST : (i + 1) * BURST], lent)
 
         def sub_silu(tiles, between):
             reads = [(t, w) for t in tiles for w in range(W)]
@@ -236,10 +253,10 @@ def tile_dendriticlayersilu_ffn_kernel(tc, x, template_flat_bytes, template_flat
 
         clock_work = keep.tile([P, N], BF16, name="clock_work")
         nc.vector.memset(clock_work[:], 0.0)
-        nc.sync.dma_start(out=scales4[:], in_=template_flat_scale.rearrange("o (g p e) -> p (o g) e", p=P, e=4))
-        load_bytes(0)
+        nc.scalar.dma_start(out=scales4[:], in_=template_flat_scale.rearrange("o (g p e) -> p (o g) e", p=P, e=4))
+        load_bytes(0, pieces=4)
+        load_bytes(1, pieces=2)
         load_x(0, 0)
-        load_bytes(1)
         load_x(0, 1)
         load_x(1, 0)
         load_x(1, 1)

@@ -24,7 +24,7 @@ NT = N // P
 BATCH = 2
 BURST = 4
 NB = HT // BATCH
-G_SHARE = 2560
+G_SHARE = 512
 
 
 def tile_dendriticlayersilu_ffn_kernel(tc, x, template_flat_bytes, template_flat_scale, out):
@@ -54,6 +54,7 @@ def tile_dendriticlayersilu_ffn_kernel(tc, x, template_flat_bytes, template_flat
         t_codes = {}
         t_scales = {}
         run = {}
+        s0 = {}
         f = {}
         d = {}
         acc_d = {}
@@ -152,7 +153,7 @@ def tile_dendriticlayersilu_ffn_kernel(tc, x, template_flat_bytes, template_flat
             rest = queue[ahead:]
             for t in before:
                 finish(t)
-            for i in range(len(reads) // BURST):
+            for i in range((len(reads) + BURST - 1) // BURST):
                 for t, w in reads[i * BURST : (i + 1) * BURST]:
                     read(t, w, bank_of[(name, t, w)])
                 units(between[i])
@@ -160,16 +161,20 @@ def tile_dendriticlayersilu_ffn_kernel(tc, x, template_flat_bytes, template_flat
 
         def read_max(t, w, bank):
             if w == 0:
-                if t not in run:
-                    run[t] = small.tile([P, N], F32, name="run", bufs=4)
-                    nc.scalar.copy(out=run[t][:], in_=bank[:])
+                if t not in s0:
+                    s0[t] = small.tile([P, N], F32, name="s0", bufs=2)
+                    nc.scalar.copy(out=s0[t][:], in_=bank[:])
+            elif w == 1:
+                run[t] = small.tile([P, N], F32, name="run", bufs=4)
+                nc.vector.tensor_tensor(out=run[t][:], in0=bank[:], in1=s0[t][:], op=ALU.max)
             else:
                 nc.vector.tensor_tensor(out=run[t][:], in0=bank[:], in1=run[t][:], op=ALU.max)
 
         def read_sub_silu(t, w, bank):
-            if w == 0:
+            if w == 1:
                 f[t] = work.tile([P, W, N], F32, name="f", bufs=4, align_bytes=64)
                 d[t] = work.tile([P, W, N], F32, name="d", align_bytes=64)
+                nc.scalar.activation(out=f[t][:, 0, :], in_=s0[t][:], func=ACT.Silu)
             nc.vector.tensor_tensor(out=d[t][:, w, :], in0=bank[:], in1=run[t][:], op=ALU.subtract)
             nc.scalar.activation(out=f[t][:, w, :], in_=bank[:], func=ACT.Silu)
 
@@ -181,7 +186,7 @@ def tile_dendriticlayersilu_ffn_kernel(tc, x, template_flat_bytes, template_flat
                 reads.extend([(first, w + 1), (second, w + 1), (first, w), (second, w)])
                 queue.extend([("max", second, w), ("max", second, w + 1), ("max", first, w), ("max", first, w + 1)])
             lent = [key for j, key in enumerate(queue) if j % 7 >= 5]
-            queue.append(("sub", first, 0))
+            queue.append(("sub", first, 1))
             return reads, queue, lent
 
         def max_start(tiles):
@@ -204,8 +209,10 @@ def tile_dendriticlayersilu_ffn_kernel(tc, x, template_flat_bytes, template_flat
                 issue(rest[i * BURST : (i + 1) * BURST], lent)
 
         def sub_silu(tiles, between):
-            reads = [(t, w) for t in tiles for w in range(W)]
+            reads = [(t, w) for t in tiles for w in range(1, W)]
             score_pass("sub", reads, [("sub", t, w) for t, w in reads[1:]], read_sub_silu, between, [])
+            for t in tiles:
+                nc.gpsimd.tensor_tensor(out=d[t][:, 0, :], in0=s0[t][:], in1=run[t][:], op=ALU.subtract)
 
         def exp_pass(t, cuts):
             for lo, hi in zip(cuts[:-1], cuts[1:]):

@@ -163,7 +163,10 @@ def tile_dendriticlayersilu_ffn_kernel(tc, x, template_flat_bytes, template_flat
             if w == 0:
                 if t not in s0:
                     s0[t] = small.tile([P, N], F32, name="s0", bufs=2)
-                    nc.scalar.copy(out=s0[t][:], in_=bank[:])
+                    if t % BATCH == 0 and t >= BATCH:
+                        nc.vector.tensor_copy(out=s0[t][:], in_=bank[:])
+                    else:
+                        nc.scalar.copy(out=s0[t][:], in_=bank[:])
             elif w == 1:
                 run[t] = small.tile([P, N], F32, name="run", bufs=4)
                 nc.vector.tensor_tensor(out=run[t][:], in0=bank[:], in1=s0[t][:], op=ALU.max)

@@ -62,6 +62,7 @@ def tile_dendriticlayersilu_ffn_kernel(tc, x, template_flat_bytes, template_flat
         ln_d = {}
         r_d = {}
         bank_of = {}
+        turned = {}
 
         def load_bytes(t, pieces=1):
             tb[t] = stage.tile([P, W * K], U8, name="tb", bufs=4)
@@ -92,17 +93,22 @@ def tile_dendriticlayersilu_ffn_kernel(tc, x, template_flat_bytes, template_flat
                 else:
                     nc.scalar.copy(out=dst(q), in_=bank[:])
 
+        def turn_bank(t, q):
+            words = wb[t][:].bitcast(F32)
+            turned[(t, q)] = psum.tile([P, 2, P, 2], F32, name="rot")
+            for gg in range(2):
+                g = 2 * q + gg
+                for u in range(2):
+                    nc.tensor.transpose(turned[(t, q)][:, gg, :, u], words[:, 256 * g + u : 256 * (g + 1) : 2], ident[:])
+
         def evac(t, banks):
             if t not in grouped:
                 grouped[t] = stage.tile([P, W * K], BF16, name="grouped", bufs=2, align_bytes=64)
             g_vals = grouped[t][:].rearrange("p (g r e) -> p g r e", g=W, e=4)
-            words = wb[t][:].bitcast(F32)
             for q in banks:
-                bank = psum.tile([P, 2, P, 2], F32, name="rot")
-                for gg in range(2):
-                    g = 2 * q + gg
-                    for u in range(2):
-                        nc.tensor.transpose(bank[:, gg, :, u], words[:, 256 * g + u : 256 * (g + 1) : 2], ident[:])
+                if (t, q) not in turned:
+                    turn_bank(t, q)
+                bank = turned[(t, q)]
                 nc.vector.tensor_tensor(
                     out=g_vals[:, 2 * q : 2 * q + 2, :, :],
                     in0=bank[:].rearrange("p g r u -> p (g r u)").bitcast(BF16).rearrange("p (g r e) -> p g r e", g=2, e=4),
@@ -130,7 +136,9 @@ def tile_dendriticlayersilu_ffn_kernel(tc, x, template_flat_bytes, template_flat
             for kind, t, nb in todo:
                 if t < 0 or t >= HT:
                     continue
-                if kind == "d":
+                if kind == "turn":
+                    turn_bank(t, nb)
+                elif kind == "d":
                     if nb == 0:
                         acc_d[t] = psum.tile([P, N], F32, name="acc", bufs=3)
                     window_sum(acc_d[t], d[t], nb)
@@ -320,7 +328,7 @@ def tile_dendriticlayersilu_ffn_kernel(tc, x, template_flat_bytes, template_flat
                     load_bytes(t)
             sub_silu(
                 cur,
-                [[("n", t0 - 2, nb)] for nb in range(NT)],
+                [[("n", t0 - 2, nb)] for nb in range(NT - 1)] + [[("turn", t0 + 2, 0), ("n", t0 - 2, NT - 1)]],
             )
             if b + 1 >= NB:
                 divide(t0 - 2)

@@ -140,12 +140,17 @@ def tile_dendriticlayersilu_ffn_kernel(tc, x, template_flat_bytes, template_flat
                     turn_bank(t, nb)
                 elif kind == "d":
                     if nb == 0:
-                        acc_d[t] = psum.tile([P, N], F32, name="acc", bufs=3)
+                        acc_d[t] = sum_bank(t >= HT - 1)
                     window_sum(acc_d[t], d[t], nb)
                 else:
                     if nb == 0:
-                        acc_n[t] = psum.tile([P, N], F32, name="acc", bufs=3)
+                        acc_n[t] = sum_bank(t >= HT - 3)
                     window_sum(acc_n[t], f[t], nb)
+
+        def sum_bank(late):
+            if late:
+                return psum.tile([P, N], F32, name="rot")
+            return psum.tile([P, N], F32, name="acc", bufs=3)
 
         def issue(keys, lent=()):
             for key in keys:
@@ -256,7 +261,7 @@ def tile_dendriticlayersilu_ffn_kernel(tc, x, template_flat_bytes, template_flat
             nc.vector.reciprocal(out=r_d[t][:], in_=acc_d[t][:])
 
         def finish(t):
-            o = small.tile([P, N], F32, name="o")
+            o = small.tile([P, N], F32, name="o", bufs=3)
             nc.vector.tensor_tensor(out=o[:], in0=acc_n[t][:], in1=r_d[t][:], op=ALU.mult)
             nc.sync.dma_start(out=out_view[:, :, t * P : (t + 1) * P], in_=o[:].rearrange("p (nb h) -> p nb h", nb=NT))
 
@@ -350,10 +355,7 @@ def tile_dendriticlayersilu_ffn_kernel(tc, x, template_flat_bytes, template_flat
                     nc.vector.tensor_copy(out=seen_by_vector[:], in_=wb[batches[b + 2][1]][:, G_SHARE - 1 : G_SHARE])
                 for t in batches[b + 1]:
                     quant(t)
-            if b + 1 >= NB:
-                divide(t0 - 1)
-                finish(t0 - 1)
-            elif b >= 1:
+            if b >= 1 and b + 1 < NB:
                 log_pass([t0 - 1])
                 exp_pass(cur[0], [0, 128])
                 recip_pass(batches[b - 1])
@@ -386,7 +388,11 @@ def tile_dendriticlayersilu_ffn_kernel(tc, x, template_flat_bytes, template_flat
                         engine = nc.gpsimd if (t == cur[0] and nb < 2) else nc.vector
                         engine.tensor_tensor(out=f[t][:, :, bs], in0=f[t][:, :, bs], in1=d[t][:, :, bs], op=ALU.mult)
                         units([("n", t, nb)])
-        log_pass(batches[NB - 1])
-        recip_pass(batches[NB - 1])
-        for t in batches[NB - 1]:
-            finish(t)
+        for group in ([HT - 3, HT - 2], [HT - 1]):
+            for t in group:
+                ln_d[t] = small.tile([P, N], F32, name="ln_d")
+                nc.scalar.activation(out=ln_d[t][:], in_=acc_d[t][:], func=ACT.Abs_reciprocal_sqrt)
+            for t in group:
+                r_d[t] = small.tile([P, N], F32, name="r_d")
+                nc.scalar.activation(out=r_d[t][:], in_=ln_d[t][:], func=ACT.Square)
+                finish(t)

@@ -93,9 +93,14 @@ def tile_dendriticlayersilu_ffn_kernel(tc, x, template_flat_bytes, template_flat
                 else:
                     nc.scalar.copy(out=dst(q), in_=bank[:])
 
-        def turn_bank(t, q):
+        def turn_bank(t, q, lent=False):
             words = wb[t][:].bitcast(F32)
-            turned[(t, q)] = psum.tile([P, 2, P, 2], F32, name="rot")
+            if lent:
+                turned[(t, q)] = psum.tile([P, 2, P, 2], F32, name="acc", bufs=3)
+            else:
+                turned[(t, q)] = psum.tile([P, 2, P, 2], F32, name="rot")
+            if t not in grouped:
+                grouped[t] = stage.tile([P, W * K], BF16, name="grouped", bufs=2, align_bytes=64)
             for gg in range(2):
                 g = 2 * q + gg
                 for u in range(2):
@@ -115,6 +120,20 @@ def tile_dendriticlayersilu_ffn_kernel(tc, x, template_flat_bytes, template_flat
                     in1=scales4[:, 2 * q : 2 * q + 2, :].unsqueeze(2).to_broadcast([P, 2, P, 4]),
                     op=ALU.mult,
                 )
+
+        def copy_words(t, q):
+            nc.scalar.copy(
+                out=grouped[t][:].bitcast(F32).rearrange("p (g r u) -> p g r u", g=W, u=2)[:, 2 * q : 2 * q + 2, :, :], in_=turned[(t, q)][:]
+            )
+
+        def scale_in_place(t, q):
+            g_vals = grouped[t][:].rearrange("p (g r e) -> p g r e", g=W, e=4)
+            nc.gpsimd.tensor_tensor(
+                out=g_vals[:, 2 * q : 2 * q + 2, :, :],
+                in0=g_vals[:, 2 * q : 2 * q + 2, :, :],
+                in1=scales4[:, 2 * q : 2 * q + 2, :].unsqueeze(2).to_broadcast([P, 2, P, 4]),
+                op=ALU.mult,
+            )
 
         def quant(t):
             t_codes[t] = stage.tile([P, W * P], U32, name="t_codes", bufs=4, align_bytes=64)
@@ -277,19 +296,22 @@ def tile_dendriticlayersilu_ffn_kernel(tc, x, template_flat_bytes, template_flat
         clock_work = keep.tile([P, N], BF16, name="clock_work")
         nc.vector.memset(clock_work[:], 0.0)
         nc.scalar.dma_start(out=scales4[:], in_=template_flat_scale.rearrange("o (g p e) -> p (o g) e", p=P, e=4))
+        table_work = keep.tile([P, 1], F32, name="table_work")
+        nc.scalar.activation(out=table_work[:], in_=clock_work[:, 0:1], func=ACT.Silu)
         load_bytes(0, pieces=4)
         load_bytes(1, pieces=2)
+        load_bytes(2)
         load_x(0, 0)
         load_x(0, 1)
         load_x(1, 0)
         load_x(1, 1)
-        load_bytes(2)
         load_bytes(3)
         unread = psum.tile([P, N], F32, name="rot")
         for i in range(5):
             nc.tensor.matmul(out=unread[:], lhsT=clock_work[:, 0:P], rhs=clock_work[:], start=True, stop=True)
         cast(0, [("s", 0, 1024), ("g", 2048, 3072), ("s", 1024, 2048), ("g", 3072, 4096)])
         cast(1, [("s", 0, 1024), ("g", 2048, 3072), ("s", 1024, 2048), ("g", 3072, 4096)])
+        cast(2, [("g", 0, 2048), ("g", 2048, 4096)])
         load_bytes(4)
         load_bytes(5)
         x_grouped = []
@@ -316,13 +338,25 @@ def tile_dendriticlayersilu_ffn_kernel(tc, x, template_flat_bytes, template_flat
 
         evac(0, range(W // 2))
         evac(1, range(W // 2))
+        nc.vector.tensor_copy(out=seen_by_vector[:], in_=wb[2][:, W * K - 1 : W * K])
         quant(0)
         quant(1)
         prepare_x(0)
         prepare_x(1)
+        for q in range(2):
+            turn_bank(2, q)
+            copy_words(2, q)
+        for q in range(2, 3):
+            turn_bank(2, q, lent=True)
         nc.gpsimd.tensor_copy(out=seen_by_gpsimd[:], in_=x_codes[:, W * N - 1 : W * N])
-        cast(2, [("g", 0, W * K)])
+        max_start(batches[0])
+        for q in range(2, 3):
+            copy_words(2, q)
+        for q in range(3):
+            scale_in_place(2, q)
         cast(3, [("g", 0, W * K)])
+        wb[5] = stage.tile([P, W * K], BF16, name="wb", bufs=3)
+        nc.scalar.copy(out=wb[5][:, G_SHARE:], in_=tb[5][:, G_SHARE:].bitcast(FP8))
         max_pass(batches[0], [[], [], [], []], [])
 
         for b in range(NB):
@@ -333,7 +367,7 @@ def tile_dendriticlayersilu_ffn_kernel(tc, x, template_flat_bytes, template_flat
                     load_bytes(t)
             sub_silu(
                 cur,
-                [[("n", t0 - 2, nb)] for nb in range(NT - 1)] + [[("turn", t0 + 2, 0), ("n", t0 - 2, NT - 1)]],
+                [[("n", t0 - 2, nb)] for nb in range(NT - 1)] + [[("turn", t0 + 2, 0 if b >= 1 else 3), ("n", t0 - 2, NT - 1)]],
             )
             if b + 1 >= NB:
                 divide(t0 - 2)
@@ -342,9 +376,12 @@ def tile_dendriticlayersilu_ffn_kernel(tc, x, template_flat_bytes, template_flat
                 log_pass([t0 - 2])
             if b + 2 < NB:
                 cast(batches[b + 2][0], [("g", 0, W * K)])
-                cast(batches[b + 2][1], [("g", 0, G_SHARE), ("s", G_SHARE, W * K)])
+                if b >= 1:
+                    cast(batches[b + 2][1], [("g", 0, G_SHARE), ("s", G_SHARE, W * K)])
+                else:
+                    nc.gpsimd.tensor_copy(out=wb[5][:, 0:G_SHARE], in_=tb[5][:, 0:G_SHARE].bitcast(FP8))
             if b + 1 < NB:
-                evac(batches[b + 1][0], range(W // 2))
+                evac(batches[b + 1][0], range(0 if b >= 1 else 3, W // 2))
                 evac(batches[b + 1][1], [0])
             units([("d", t0 - 1, nb) for nb in range(NT)])
             if b + 1 < NB:

@@ -25,6 +25,7 @@ BATCH = 2
 BURST = 4
 NB = HT // BATCH
 G_SHARE = 512
+S_CUTS = [G_SHARE, 1536, 2816, W * K]
 
 
 def tile_dendriticlayersilu_ffn_kernel(tc, x, template_flat_bytes, template_flat_scale, out):
@@ -157,6 +158,13 @@ def tile_dendriticlayersilu_ffn_kernel(tc, x, template_flat_bytes, template_flat
                     continue
                 if kind == "turn":
                     turn_bank(t, nb)
+                elif kind == "past":
+                    turn_bank(t, nb, lent=True)
+                    copy_words(t, nb)
+                    scale_in_place(t, nb)
+                elif kind == "share":
+                    lo, hi = S_CUTS[nb], S_CUTS[nb + 1]
+                    nc.scalar.copy(out=wb[t][:, lo:hi], in_=tb[t][:, lo:hi].bitcast(FP8))
                 elif kind == "d":
                     if nb == 0:
                         acc_d[t] = sum_bank(t >= HT - 1)
@@ -309,7 +317,7 @@ def tile_dendriticlayersilu_ffn_kernel(tc, x, template_flat_bytes, template_flat
         unread = psum.tile([P, N], F32, name="rot")
         for i in range(5):
             nc.tensor.matmul(out=unread[:], lhsT=clock_work[:, 0:P], rhs=clock_work[:], start=True, stop=True)
-        cast(0, [("s", 0, 1024), ("g", 2048, 3072), ("s", 1024, 2048), ("g", 3072, 4096)])
+        cast(0, [("v", 0, 1024), ("s", 1024, 2048), ("g", 2048, 3072), ("s", 3072, 4096)])
         cast(1, [("s", 0, 1024), ("g", 2048, 3072), ("s", 1024, 2048), ("g", 3072, 4096)])
         cast(2, [("g", 0, 2048), ("g", 2048, 4096)])
         load_bytes(4)
@@ -343,21 +351,14 @@ def tile_dendriticlayersilu_ffn_kernel(tc, x, template_flat_bytes, template_flat
         quant(1)
         prepare_x(0)
         prepare_x(1)
-        for q in range(2):
-            turn_bank(2, q)
-            copy_words(2, q)
-        for q in range(2, 3):
-            turn_bank(2, q, lent=True)
+        turn_bank(2, 0)
+        copy_words(2, 0)
         nc.gpsimd.tensor_copy(out=seen_by_gpsimd[:], in_=x_codes[:, W * N - 1 : W * N])
         max_start(batches[0])
-        for q in range(2, 3):
-            copy_words(2, q)
-        for q in range(3):
-            scale_in_place(2, q)
-        cast(3, [("g", 0, W * K)])
+        scale_in_place(2, 0)
         wb[5] = stage.tile([P, W * K], BF16, name="wb", bufs=3)
-        nc.scalar.copy(out=wb[5][:, G_SHARE:], in_=tb[5][:, G_SHARE:].bitcast(FP8))
-        max_pass(batches[0], [[], [], [], []], [])
+        max_pass(batches[0], [[("past", 2, 1), ("share", 5, 0)], [("past", 2, 2), ("share", 5, 1)], [("share", 5, 2)], []], [])
+        cast(3, [("g", 0, W * K)])
 
         for b in range(NB):
             cur = batches[b]
@@ -367,8 +368,14 @@ def tile_dendriticlayersilu_ffn_kernel(tc, x, template_flat_bytes, template_flat
                     load_bytes(t)
             sub_silu(
                 cur,
-                [[("n", t0 - 2, nb)] for nb in range(NT - 1)] + [[("turn", t0 + 2, 0 if b >= 1 else 3), ("n", t0 - 2, NT - 1)]],
+                [[("n", t0 - 2, nb) if b != NB - 2 else ("d", t0 - 1, nb)] for nb in range(NT - 1)]
+                + [[("turn", t0 + 2, 0 if b >= 1 else 3), ("n", t0 - 2, NT - 1) if b != NB - 2 else ("d", t0 - 1, NT - 1)]],
             )
+            if b == NB - 2:
+                for q in range(1):
+                    turn_bank(t0 + 3, q)
+                    copy_words(t0 + 3, q)
+                    scale_in_place(t0 + 3, q)
             if b + 1 >= NB:
                 divide(t0 - 2)
                 finish(t0 - 2)
@@ -382,14 +389,16 @@ def tile_dendriticlayersilu_ffn_kernel(tc, x, template_flat_bytes, template_flat
                     nc.gpsimd.tensor_copy(out=wb[5][:, 0:G_SHARE], in_=tb[5][:, 0:G_SHARE].bitcast(FP8))
             if b + 1 < NB:
                 evac(batches[b + 1][0], range(0 if b >= 1 else 3, W // 2))
-                evac(batches[b + 1][1], [0])
-            units([("d", t0 - 1, nb) for nb in range(NT)])
+                evac(batches[b + 1][1], [0] if b < NB - 2 else [1])
+            units([("d", t0 - 1, nb) if b != NB - 2 else ("n", t0 - 2, nb) for nb in range(NT)])
             if b + 1 < NB:
-                evac(batches[b + 1][1], range(1, W // 2))
+                evac(batches[b + 1][1], range(1 if b < NB - 2 else 2, W // 2))
             units([("n", t0 - 1, nb) for nb in range(NT)])
             if b + 1 < NB:
                 if b + 2 < NB:
                     nc.vector.tensor_copy(out=seen_by_vector[:], in_=wb[batches[b + 2][1]][:, G_SHARE - 1 : G_SHARE])
+                if b == NB - 2:
+                    nc.vector.tensor_copy(out=seen_by_vector[:], in_=grouped[t0 + 3][:, 1 * 2 * K - 1 : 1 * 2 * K])
                 for t in batches[b + 1]:
                     quant(t)
             if b >= 1 and b + 1 < NB:

@@ -368,8 +368,8 @@ def tile_dendriticlayersilu_ffn_kernel(tc, x, template_flat_bytes, template_flat
                     load_bytes(t)
             sub_silu(
                 cur,
-                [[("n", t0 - 2, nb) if b != NB - 2 else ("d", t0 - 1, nb)] for nb in range(NT - 1)]
-                + [[("turn", t0 + 2, 0 if b >= 1 else 3), ("n", t0 - 2, NT - 1) if b != NB - 2 else ("d", t0 - 1, NT - 1)]],
+                [[("n", t0 - 2, nb) if b != NB - 2 else ("d", t0 - 1, nb)] if (nb < 2 or b >= NB - 2) else [] for nb in range(NT - 1)]
+                + [[("turn", t0 + 2, 0 if b >= 1 else 3)] + ([("n", t0 - 2, NT - 1) if b != NB - 2 else ("d", t0 - 1, NT - 1)] if b >= NB - 2 else [])],
             )
             if b == NB - 2:
                 for q in range(1):
@@ -393,6 +393,8 @@ def tile_dendriticlayersilu_ffn_kernel(tc, x, template_flat_bytes, template_flat
             units([("d", t0 - 1, nb) if b != NB - 2 else ("n", t0 - 2, nb) for nb in range(NT)])
             if b + 1 < NB:
                 evac(batches[b + 1][1], range(1 if b < NB - 2 else 2, W // 2))
+            if b < NB - 2:
+                units([("n", t0 - 2, nb) for nb in range(2, NT)])
             units([("n", t0 - 1, nb) for nb in range(NT)])
             if b + 1 < NB:
                 if b + 2 < NB:

@@ -421,7 +421,7 @@ def tile_dendriticlayersilu_ffn_kernel(tc, x, template_flat_bytes, template_flat
                 exp_pass(cur[1], [0, 256, 512])
             if b + 1 < NB:
                 nc.gpsimd.tensor_copy(out=seen_by_gpsimd[:], in_=t_codes[t0 + 3][:, W * P - 1 : W * P])
-                for t, cuts in ((cur[0], [0, 128, 256, 512]), (cur[1], [0, 256, 512])):
+                for t, cuts in ((cur[0], [0, 256, 512]), (cur[1], [0, 512])):
                     for lo, hi in zip(cuts[:-1], cuts[1:]):
                         nc.gpsimd.tensor_tensor(out=f[t][:, :, lo:hi], in0=f[t][:, :, lo:hi], in1=d[t][:, :, lo:hi], op=ALU.mult)
                 sums_in_max_pass = [[("d", t0, nb)] for nb in range(NT)]

@@ -25,7 +25,7 @@ BATCH = 2
 BURST = 4
 NB = HT // BATCH
 G_SHARE = 512
-S_CUTS = [G_SHARE, 1536, 2816, W * K]
+S_CUTS = [0, 1280, 2688, W * K]
 
 
 def tile_dendriticlayersilu_ffn_kernel(tc, x, template_flat_bytes, template_flat_scale, out):
@@ -384,9 +384,7 @@ def tile_dendriticlayersilu_ffn_kernel(tc, x, template_flat_bytes, template_flat
             if b + 2 < NB:
                 cast(batches[b + 2][0], [("g", 0, W * K)])
                 if b >= 1:
-                    cast(batches[b + 2][1], [("g", 0, G_SHARE), ("s", G_SHARE, W * K)])
-                else:
-                    nc.gpsimd.tensor_copy(out=wb[5][:, 0:G_SHARE], in_=tb[5][:, 0:G_SHARE].bitcast(FP8))
+                    cast(batches[b + 2][1], [("s", 0, W * K)])
             if b + 1 < NB:
                 evac(batches[b + 1][0], range(0 if b >= 1 else 3, W // 2))
                 evac(batches[b + 1][1], [0] if b < NB - 2 else [1])
@@ -398,7 +396,7 @@ def tile_dendriticlayersilu_ffn_kernel(tc, x, template_flat_bytes, template_flat
             units([("n", t0 - 1, nb) for nb in range(NT)])
             if b + 1 < NB:
                 if b + 2 < NB:
-                    nc.vector.tensor_copy(out=seen_by_vector[:], in_=wb[batches[b + 2][1]][:, G_SHARE - 1 : G_SHARE])
+                    nc.vector.tensor_copy(out=seen_by_vector[:], in_=wb[batches[b + 2][0]][:, W * K - 1 : W * K])
                 if b == NB - 2:
                     nc.vector.tensor_copy(out=seen_by_vector[:], in_=grouped[t0 + 3][:, 1 * 2 * K - 1 : 1 * 2 * K])
                 for t in batches[b + 1]:

@@ -395,8 +395,6 @@ def tile_dendriticlayersilu_ffn_kernel(tc, x, template_flat_bytes, template_flat
                 units([("n", t0 - 2, nb) for nb in range(2, NT)])
             units([("n", t0 - 1, nb) for nb in range(NT)])
             if b + 1 < NB:
-                if b + 2 < NB:
-                    nc.vector.tensor_copy(out=seen_by_vector[:], in_=wb[batches[b + 2][0]][:, W * K - 1 : W * K])
                 if b == NB - 2:
                     nc.vector.tensor_copy(out=seen_by_vector[:], in_=grouped[t0 + 3][:, 1 * 2 * K - 1 : 1 * 2 * K])
                 for t in batches[b + 1]:
@@ -434,7 +432,7 @@ def tile_dendriticlayersilu_ffn_kernel(tc, x, template_flat_bytes, template_flat
                         engine = nc.gpsimd if (t == cur[0] and nb < 2) else nc.vector
                         engine.tensor_tensor(out=f[t][:, :, bs], in0=f[t][:, :, bs], in1=d[t][:, :, bs], op=ALU.mult)
                         units([("n", t, nb)])
-        for group in ([HT - 3, HT - 2], [HT - 1]):
+        for group in ([HT - 3, HT - 2],):
             for t in group:
                 ln_d[t] = small.tile([P, N], F32, name="ln_d")
                 nc.scalar.activation(out=ln_d[t][:], in_=acc_d[t][:], func=ACT.Abs_reciprocal_sqrt)
@@ -442,3 +440,16 @@ def tile_dendriticlayersilu_ffn_kernel(tc, x, template_flat_bytes, template_flat
                 r_d[t] = small.tile([P, N], F32, name="r_d")
                 nc.scalar.activation(out=r_d[t][:], in_=ln_d[t][:], func=ACT.Square)
                 finish(t)
+        t = HT - 1
+        ln_d[t] = small.tile([P, N], F32, name="ln_d")
+        r_d[t] = small.tile([P, N], F32, name="r_d")
+        o_last = small.tile([P, N], F32, name="o", bufs=3)
+        for half in range(2):
+            hs = slice(half * N // 2, (half + 1) * N // 2)
+            nc.scalar.activation(out=ln_d[t][:, hs], in_=acc_d[t][:, hs], func=ACT.Abs_reciprocal_sqrt)
+            nc.scalar.activation(out=r_d[t][:, hs], in_=ln_d[t][:, hs], func=ACT.Square)
+            nc.vector.tensor_tensor(out=o_last[:, hs], in0=acc_n[t][:, hs], in1=r_d[t][:, hs], op=ALU.mult)
+            nc.sync.dma_start(
+                out=out_view[:, half * NT // 2 : (half + 1) * NT // 2, t * P : (t + 1) * P],
+                in_=o_last[:, hs].rearrange("p (nb h) -> p nb h", nb=NT // 2),
+            )

@@ -40,8 +40,8 @@ def tile_dendriticlayersilu_ffn_kernel(tc, x, template_flat_bytes, template_flat
 
         ident = keep.tile([P, P], F32, name="ident")
         make_identity(nc, ident[:])
-        x_codes = keep.tile([P, W * N], U32, name="x_codes", align_bytes=64)
-        x_scales = keep.tile([P, W * N], U8, name="x_scales", align_bytes=64)
+        x_codes = keep.tile([P, W * N], U32, name="x_codes", align_bytes=256)
+        x_scales = keep.tile([P, W * N], U8, name="x_scales", align_bytes=256)
         scales4 = keep.tile([P, W, 4], F32, name="scales4")
         seen_by_vector = keep.tile([P, 1], F32, name="seen_by_vector")
         seen_by_gpsimd = keep.tile([P, 1], U32, name="seen_by_gpsimd")
@@ -137,8 +137,8 @@ def tile_dendriticlayersilu_ffn_kernel(tc, x, template_flat_bytes, template_flat
             )
 
         def quant(t):
-            t_codes[t] = stage.tile([P, W * P], U32, name="t_codes", bufs=4, align_bytes=64)
-            t_scales[t] = stage.tile([P, W * P], U8, name="t_scales", bufs=4, align_bytes=64)
+            t_codes[t] = stage.tile([P, W * P], U32, name="t_codes", bufs=4, align_bytes=256)
+            t_scales[t] = stage.tile([P, W * P], U8, name="t_scales", bufs=4, align_bytes=256)
             nc.vector.quantize_mx(out=t_codes[t][:].bitcast(FP8X4), scales=t_scales[t][:], in_=grouped[t][:])
 
         def scores(bank, t, w):

from contextlib import ExitStack

import concourse.mybir as mybir
from concourse.masks import make_identity

N = 512
H = 2048
W = 8
K = 512
P = 128
FLOPS = 2 * N * H * W * K

F32 = mybir.dt.float32
BF16 = mybir.dt.bfloat16
U32 = mybir.dt.uint32
U8 = mybir.dt.uint8
FP8 = mybir.dt.float8_e4m3fn
FP8X4 = mybir.dt.float8_e4m3fn_x4
ACT = mybir.ActivationFunctionType
ALU = mybir.AluOpType

HT = H // P
NT = N // P
BATCH = 2
BURST = 4
NB = HT // BATCH
G_SHARE = 512
S_CUTS = [0, 1280, 2688, W * K]


def tile_dendriticlayersilu_ffn_kernel(tc, x, template_flat_bytes, template_flat_scale, out):
    nc = tc.nc
    with ExitStack() as ctx:
        keep = ctx.enter_context(tc.tile_pool(name="keep", bufs=1))
        stage = ctx.enter_context(tc.tile_pool(name="stage", bufs=2))
        work = ctx.enter_context(tc.tile_pool(name="work", bufs=3))
        small = ctx.enter_context(tc.tile_pool(name="small", bufs=2))
        psum = ctx.enter_context(tc.psum_pool(name="psum", bufs=5))
        ctx.enter_context(tc.manual_schedule(engines={mybir.EngineType.Activation, mybir.EngineType.DVE, mybir.EngineType.Pool, mybir.EngineType.PE}))

        ident = keep.tile([P, P], F32, name="ident")
        make_identity(nc, ident[:])
        x_codes = keep.tile([P, W * N], U32, name="x_codes", align_bytes=256)
        x_scales = keep.tile([P, W * N], U8, name="x_scales", align_bytes=256)
        scales4 = keep.tile([P, W, 4], F32, name="scales4")
        seen_by_vector = keep.tile([P, 1], F32, name="seen_by_vector")
        seen_by_gpsimd = keep.tile([P, 1], U32, name="seen_by_gpsimd")

        out_view = out.rearrange("(nb p) h -> p nb h", p=P)
        x_view = x.rearrange("(i p) k -> p i k", p=P)
        batches = [list(range(b * BATCH, (b + 1) * BATCH)) for b in range(NB)]
        tb = {}
        wb = {}
        grouped = {}
        t_codes = {}
        t_scales = {}
        run = {}
        s0 = {}
        f = {}
        d = {}
        acc_d = {}
        acc_n = {}
        ln_d = {}
        r_d = {}
        bank_of = {}
        turned = {}

        def load_bytes(t, pieces=1):
            tb[t] = stage.tile([P, W * K], U8, name="tb", bufs=4)
            width = W * K // pieces
            for i in range(pieces):
                cs = slice(i * width, (i + 1) * width)
                nc.sync.dma_start(out=tb[t][:, cs], in_=template_flat_bytes[t * P : (t + 1) * P, cs])

        def cast(t, shares):
            wb[t] = stage.tile([P, W * K], BF16, name="wb", bufs=3)
            for who, lo, hi in shares:
                if who == "g":
                    nc.gpsimd.tensor_copy(out=wb[t][:, lo:hi], in_=tb[t][:, lo:hi].bitcast(FP8))
                elif who == "s":
                    nc.scalar.copy(out=wb[t][:, lo:hi], in_=tb[t][:, lo:hi].bitcast(FP8))
                else:
                    nc.vector.tensor_copy(out=wb[t][:, lo:hi], in_=tb[t][:, lo:hi].bitcast(FP8))

        def turn(words, dst, banks=W // 2, vector_from=W // 2):
            for q in range(banks):
                bank = psum.tile([P, 2, P, 2], F32, name="rot")
                for gg in range(2):
                    g = 2 * q + gg
                    for u in range(2):
                        nc.tensor.transpose(bank[:, gg, :, u], words[:, 256 * g + u : 256 * (g + 1) : 2], ident[:])
                if q >= vector_from:
                    nc.vector.tensor_copy(out=dst(q), in_=bank[:])
                else:
                    nc.scalar.copy(out=dst(q), in_=bank[:])

        def turn_bank(t, q, lent=False):
            words = wb[t][:].bitcast(F32)
            if lent:
                turned[(t, q)] = psum.tile([P, 2, P, 2], F32, name="acc", bufs=3)
            else:
                turned[(t, q)] = psum.tile([P, 2, P, 2], F32, name="rot")
            if t not in grouped:
                grouped[t] = stage.tile([P, W * K], BF16, name="grouped", bufs=2, align_bytes=64)
            for gg in range(2):
                g = 2 * q + gg
                for u in range(2):
                    nc.tensor.transpose(turned[(t, q)][:, gg, :, u], words[:, 256 * g + u : 256 * (g + 1) : 2], ident[:])

        def evac(t, banks):
            if t not in grouped:
                grouped[t] = stage.tile([P, W * K], BF16, name="grouped", bufs=2, align_bytes=64)
            g_vals = grouped[t][:].rearrange("p (g r e) -> p g r e", g=W, e=4)
            for q in banks:
                if (t, q) not in turned:
                    turn_bank(t, q)
                bank = turned[(t, q)]
                nc.vector.tensor_tensor(
                    out=g_vals[:, 2 * q : 2 * q + 2, :, :],
                    in0=bank[:].rearrange("p g r u -> p (g r u)").bitcast(BF16).rearrange("p (g r e) -> p g r e", g=2, e=4),
                    in1=scales4[:, 2 * q : 2 * q + 2, :].unsqueeze(2).to_broadcast([P, 2, P, 4]),
                    op=ALU.mult,
                )

        def copy_words(t, q):
            nc.scalar.copy(
                out=grouped[t][:].bitcast(F32).rearrange("p (g r u) -> p g r u", g=W, u=2)[:, 2 * q : 2 * q + 2, :, :], in_=turned[(t, q)][:]
            )

        def scale_in_place(t, q):
            g_vals = grouped[t][:].rearrange("p (g r e) -> p g r e", g=W, e=4)
            nc.gpsimd.tensor_tensor(
                out=g_vals[:, 2 * q : 2 * q + 2, :, :],
                in0=g_vals[:, 2 * q : 2 * q + 2, :, :],
                in1=scales4[:, 2 * q : 2 * q + 2, :].unsqueeze(2).to_broadcast([P, 2, P, 4]),
                op=ALU.mult,
            )

        def quant(t):
            t_codes[t] = stage.tile([P, W * P], U32, name="t_codes", bufs=4, align_bytes=256)
            t_scales[t] = stage.tile([P, W * P], U8, name="t_scales", bufs=4, align_bytes=256)
            nc.vector.quantize_mx(out=t_codes[t][:].bitcast(FP8X4), scales=t_scales[t][:], in_=grouped[t][:])

        def scores(bank, t, w):
            nc.tensor.matmul_mx(
                out=bank[:],
                lhsT=t_codes[t][:, w * P : (w + 1) * P].bitcast(FP8X4),
                lhsT_scale=t_scales[t][:, w * P : (w + 1) * P],
                rhs=x_codes[:, w * N : (w + 1) * N].bitcast(FP8X4),
                rhs_scale=x_scales[:, w * N : (w + 1) * N],
                start=True,
                stop=True,
            )

        def units(todo):
            for kind, t, nb in todo:
                if t < 0 or t >= HT:
                    continue
                if kind == "turn":
                    turn_bank(t, nb)
                elif kind == "past":
                    turn_bank(t, nb, lent=True)
                    copy_words(t, nb)
                    scale_in_place(t, nb)
                elif kind == "share":
                    lo, hi = S_CUTS[nb], S_CUTS[nb + 1]
                    nc.scalar.copy(out=wb[t][:, lo:hi], in_=tb[t][:, lo:hi].bitcast(FP8))
                elif kind == "d":
                    if nb == 0:
                        acc_d[t] = sum_bank(t >= HT - 1)
                    window_sum(acc_d[t], d[t], nb)
                else:
                    if nb == 0:
                        acc_n[t] = sum_bank(t >= HT - 3)
                    window_sum(acc_n[t], f[t], nb)

        def sum_bank(late):
            if late:
                return psum.tile([P, N], F32, name="rot")
            return psum.tile([P, N], F32, name="acc", bufs=3)

        def issue(keys, lent=()):
            for key in keys:
                if key in lent:
                    bank_of[key] = psum.tile([P, N], F32, name="acc", bufs=3)
                else:
                    bank_of[key] = psum.tile([P, N], F32, name="rot")
                scores(bank_of[key], key[1], key[2])

        def score_pass(name, reads, queue, read, between, before):
            ahead = BURST + 1 - sum(1 for t, w in reads if (name, t, w) in bank_of)
            issue(queue[:ahead])
            rest = queue[ahead:]
            for t in before:
                finish(t)
            for i in range((len(reads) + BURST - 1) // BURST):
                for t, w in reads[i * BURST : (i + 1) * BURST]:
                    read(t, w, bank_of[(name, t, w)])
                units(between[i])
                issue(rest[i * BURST : (i + 1) * BURST])

        def read_max(t, w, bank):
            if w == 0:
                if t not in s0:
                    s0[t] = small.tile([P, N], F32, name="s0", bufs=2)
                    if t % BATCH == 0 and t >= BATCH:
                        nc.vector.tensor_copy(out=s0[t][:], in_=bank[:])
                    else:
                        nc.scalar.copy(out=s0[t][:], in_=bank[:])
            elif w == 1:
                run[t] = small.tile([P, N], F32, name="run", bufs=4)
                nc.vector.tensor_tensor(out=run[t][:], in0=bank[:], in1=s0[t][:], op=ALU.max)
            else:
                nc.vector.tensor_tensor(out=run[t][:], in0=bank[:], in1=run[t][:], op=ALU.max)

        def read_sub_silu(t, w, bank):
            if w == 1:
                f[t] = work.tile([P, W, N], F32, name="f", bufs=4, align_bytes=64)
                d[t] = work.tile([P, W, N], F32, name="d", align_bytes=64)
                nc.scalar.activation(out=f[t][:, 0, :], in_=s0[t][:], func=ACT.Silu)
            nc.vector.tensor_tensor(out=d[t][:, w, :], in0=bank[:], in1=run[t][:], op=ALU.subtract)
            nc.scalar.activation(out=f[t][:, w, :], in_=bank[:], func=ACT.Silu)

        def max_plan(tiles):
            first, second = tiles
            reads = [(first, 0), (second, 0), (first, 1), (second, 1)]
            queue = [("max", first, 0), ("max", first, 1), ("max", second, 0), ("max", second, 1)]
            for w in range(2, W, 2):
                reads.extend([(first, w + 1), (second, w + 1), (first, w), (second, w)])
                queue.extend([("max", second, w), ("max", second, w + 1), ("max", first, w), ("max", first, w + 1)])
            lent = [key for j, key in enumerate(queue) if j % 7 >= 5]
            queue.append(("sub", first, 1))
            return reads, queue, lent

        def max_start(tiles):
            reads, queue, lent = max_plan(tiles)
            issue(queue[: BURST + 1], lent)
            for t in tiles:
                read_max(t, 0, bank_of[("max", t, 0)])

        def max_pass(tiles, between, before):
            reads, queue, lent = max_plan(tiles)
            started = sum(1 for key in queue if key in bank_of)
            issue(queue[started : 2 * BURST], lent)
            rest = queue[2 * BURST :]
            for t in before:
                finish(t)
            for i in range(len(reads) // BURST):
                for t, w in reads[i * BURST : (i + 1) * BURST]:
                    read_max(t, w, bank_of[("max", t, w)])
                units(between[i])
                issue(rest[i * BURST : (i + 1) * BURST], lent)

        def sub_silu(tiles, between):
            reads = [(t, w) for t in tiles for w in range(1, W)]
            score_pass("sub", reads, [("sub", t, w) for t, w in reads[1:]], read_sub_silu, between, [])
            for t in tiles:
                nc.gpsimd.tensor_tensor(out=d[t][:, 0, :], in0=s0[t][:], in1=run[t][:], op=ALU.subtract)

        def exp_pass(t, cuts):
            for lo, hi in zip(cuts[:-1], cuts[1:]):
                nc.scalar.activation(out=d[t][:, :, lo:hi], in_=d[t][:, :, lo:hi], func=ACT.Exp)

        def window_sum(acc, src, nb):
            bs = slice(nb * P, (nb + 1) * P)
            for w in range(W):
                nc.tensor.matmul(
                    out=acc[:, bs],
                    lhsT=src[:, w, bs],
                    rhs=ident[:],
                    is_transpose=True,
                    start=(w == 0),
                    stop=(w == W - 1),
                )

        def log_pass(tiles):
            for t in tiles:
                ln_d[t] = small.tile([P, N], F32, name="ln_d")
                nc.scalar.activation(out=ln_d[t][:], in_=acc_d[t][:], func=ACT.Ln)

        def recip_pass(tiles):
            for t in tiles:
                r_d[t] = small.tile([P, N], F32, name="r_d")
                nc.scalar.activation(out=r_d[t][:], in_=ln_d[t][:], func=ACT.Exp, scale=-1.0)

        def divide(t):
            r_d[t] = small.tile([P, N], F32, name="r_d")
            nc.vector.reciprocal(out=r_d[t][:], in_=acc_d[t][:])

        def finish(t):
            o = small.tile([P, N], F32, name="o", bufs=3)
            nc.vector.tensor_tensor(out=o[:], in0=acc_n[t][:], in1=r_d[t][:], op=ALU.mult)
            nc.sync.dma_start(out=out_view[:, :, t * P : (t + 1) * P], in_=o[:].rearrange("p (nb h) -> p nb h", nb=NT))

        x_cols = []

        def load_x(a, c):
            if c == 0:
                x_cols.append(work.tile([P, NT, 4 * K], BF16, name="d", align_bytes=64))
            nc.sync.dma_start(
                out=x_cols[a][:, :, c * 2 * K : (c + 1) * 2 * K], in_=x_view[:, :, (2 * a + c) * 2 * K : (2 * a + c + 1) * 2 * K]
            )

        clock_work = keep.tile([P, N], BF16, name="clock_work")
        nc.vector.memset(clock_work[:], 0.0)
        nc.scalar.dma_start(out=scales4[:], in_=template_flat_scale.rearrange("o (g p e) -> p (o g) e", p=P, e=4))
        table_work = keep.tile([P, 1], F32, name="table_work")
        nc.scalar.activation(out=table_work[:], in_=clock_work[:, 0:1], func=ACT.Silu)
        load_bytes(0, pieces=4)
        load_bytes(1, pieces=2)
        load_bytes(2)
        load_x(0, 0)
        load_x(0, 1)
        load_x(1, 0)
        load_x(1, 1)
        load_bytes(3)
        unread = psum.tile([P, N], F32, name="rot")
        for i in range(5):
            nc.tensor.matmul(out=unread[:], lhsT=clock_work[:, 0:P], rhs=clock_work[:], start=True, stop=True)
        cast(0, [("v", 0, 1024), ("s", 1024, 2048), ("g", 2048, 3072), ("s", 3072, 4096)])
        cast(1, [("s", 0, 1024), ("g", 2048, 3072), ("s", 1024, 2048), ("g", 3072, 4096)])
        cast(2, [("g", 0, 2048), ("g", 2048, 4096)])
        load_bytes(4)
        load_bytes(5)
        x_grouped = []
        xg_words = []
        for a in range(2):
            xg = work.tile([P, 4 * N * 4], BF16, name="f", bufs=4, align_bytes=64)
            x_grouped.append(xg)
            xg_words.append(xg[:].bitcast(F32).rearrange("p (g n u) -> p g n u", g=4, u=2))

        def prepare_x(a):
            for c in range(2):
                for i in range(NT):
                    turn(
                        x_cols[a][:, i, c * 2 * K : (c + 1) * 2 * K].bitcast(F32),
                        lambda q: xg_words[a][:, 2 * c : 2 * c + 2, i * P : (i + 1) * P, :],
                        banks=1,
                    )
                g = 4 * a + 2 * c
                nc.vector.quantize_mx(
                    out=x_codes[:, g * N : (g + 2) * N].bitcast(FP8X4),
                    scales=x_scales[:, g * N : (g + 2) * N],
                    in_=x_grouped[a][:, c * 4096 : (c + 1) * 4096],
                )

        evac(0, range(W // 2))
        evac(1, range(W // 2))
        nc.vector.tensor_copy(out=seen_by_vector[:], in_=wb[2][:, W * K - 1 : W * K])
        quant(0)
        quant(1)
        prepare_x(0)
        prepare_x(1)
        turn_bank(2, 0)
        copy_words(2, 0)
        nc.gpsimd.tensor_copy(out=seen_by_gpsimd[:], in_=x_codes[:, W * N - 1 : W * N])
        max_start(batches[0])
        scale_in_place(2, 0)
        wb[5] = stage.tile([P, W * K], BF16, name="wb", bufs=3)
        max_pass(batches[0], [[("past", 2, 1), ("share", 5, 0)], [("past", 2, 2), ("share", 5, 1)], [("share", 5, 2)], []], [])
        cast(3, [("g", 0, W * K)])

        for b in range(NB):
            cur = batches[b]
            t0 = cur[0]
            if b + 3 < NB:
                for t in batches[b + 3]:
                    load_bytes(t)
            sub_silu(
                cur,
                [[("n", t0 - 2, nb) if b != NB - 2 else ("d", t0 - 1, nb)] if (nb < 2 or b >= NB - 2) else [] for nb in range(NT - 1)]
                + [[("turn", t0 + 2, 0 if b >= 1 else 3)] + ([("n", t0 - 2, NT - 1) if b != NB - 2 else ("d", t0 - 1, NT - 1)] if b >= NB - 2 else [])],
            )
            if b == NB - 2:
                for q in range(1):
                    turn_bank(t0 + 3, q)
                    copy_words(t0 + 3, q)
                    scale_in_place(t0 + 3, q)
            if b + 1 >= NB:
                divide(t0 - 2)
                finish(t0 - 2)
            elif b >= 1:
                log_pass([t0 - 2])
            if b + 2 < NB:
                cast(batches[b + 2][0], [("g", 0, W * K)])
                if b >= 1:
                    cast(batches[b + 2][1], [("s", 0, W * K)])
            if b + 1 < NB:
                evac(batches[b + 1][0], range(0 if b >= 1 else 3, W // 2))
                evac(batches[b + 1][1], [0] if b < NB - 2 else [1])
            units([("d", t0 - 1, nb) if b != NB - 2 else ("n", t0 - 2, nb) for nb in range(NT)])
            if b + 1 < NB:
                evac(batches[b + 1][1], range(1 if b < NB - 2 else 2, W // 2))
            if b < NB - 2:
                units([("n", t0 - 2, nb) for nb in range(2, NT)])
            units([("n", t0 - 1, nb) for nb in range(NT)])
            if b + 1 < NB:
                if b == NB - 2:
                    nc.vector.tensor_copy(out=seen_by_vector[:], in_=grouped[t0 + 3][:, 1 * 2 * K - 1 : 1 * 2 * K])
                for t in batches[b + 1]:
                    quant(t)
            if b >= 1 and b + 1 < NB:
                log_pass([t0 - 1])
                exp_pass(cur[0], [0, 128])
                recip_pass(batches[b - 1])
                exp_pass(cur[0], [128, 256, 384])
                max_start(batches[b + 1])
                exp_pass(cur[0], [384, 512])
                exp_pass(cur[1], [0, 256, 512])
            elif b == 0:
                exp_pass(cur[0], [0, 128, 256, 512])
                exp_pass(cur[1], [0, 256])
                max_start(batches[b + 1])
                exp_pass(cur[1], [256, 512])
            if b + 1 >= NB:
                exp_pass(cur[0], [0, 128, 256, 512])
                exp_pass(cur[1], [0, 256, 512])
            if b + 1 < NB:
                nc.gpsimd.tensor_copy(out=seen_by_gpsimd[:], in_=t_codes[t0 + 3][:, W * P - 1 : W * P])
                for t, cuts in ((cur[0], [0, 256, 512]), (cur[1], [0, 512])):
                    for lo, hi in zip(cuts[:-1], cuts[1:]):
                        nc.gpsimd.tensor_tensor(out=f[t][:, :, lo:hi], in0=f[t][:, :, lo:hi], in1=d[t][:, :, lo:hi], op=ALU.mult)
                sums_in_max_pass = [[("d", t0, nb)] for nb in range(NT)]
                max_pass(batches[b + 1], sums_in_max_pass, batches[b - 1] if b >= 1 else [])
            else:
                units([("d", cur[0], nb) for nb in range(NT)])
                for t in cur:
                    for nb in range(NT):
                        if t == cur[0] and nb == NT - 1:
                            units([("d", cur[1], k) for k in range(NT)])
                        bs = slice(nb * P, (nb + 1) * P)
                        engine = nc.gpsimd if (t == cur[0] and nb < 2) else nc.vector
                        engine.tensor_tensor(out=f[t][:, :, bs], in0=f[t][:, :, bs], in1=d[t][:, :, bs], op=ALU.mult)
                        units([("n", t, nb)])
        for group in ([HT - 3, HT - 2],):
            for t in group:
                ln_d[t] = small.tile([P, N], F32, name="ln_d")
                nc.scalar.activation(out=ln_d[t][:], in_=acc_d[t][:], func=ACT.Abs_reciprocal_sqrt)
            for t in group:
                r_d[t] = small.tile([P, N], F32, name="r_d")
                nc.scalar.activation(out=r_d[t][:], in_=ln_d[t][:], func=ACT.Square)
                finish(t)
        t = HT - 1
        ln_d[t] = small.tile([P, N], F32, name="ln_d")
        r_d[t] = small.tile([P, N], F32, name="r_d")
        o_last = small.tile([P, N], F32, name="o", bufs=3)
        for half in range(2):
            hs = slice(half * N // 2, (half + 1) * N // 2)
            nc.scalar.activation(out=ln_d[t][:, hs], in_=acc_d[t][:, hs], func=ACT.Abs_reciprocal_sqrt)
            nc.scalar.activation(out=r_d[t][:, hs], in_=ln_d[t][:, hs], func=ACT.Square)
            nc.vector.tensor_tensor(out=o_last[:, hs], in0=acc_n[t][:, hs], in1=r_d[t][:, hs], op=ALU.mult)
            nc.sync.dma_start(
                out=out_view[:, half * NT // 2 : (half + 1) * NT // 2, t * P : (t + 1) * P],
                in_=o_last[:, hs].rearrange("p (nb h) -> p nb h", nb=NT // 2),
            )
